import numpy as np
import ml_dtypes


def mxq(x, axis, fmt="e4m3"):
    dtype, down = {"e4m3": (ml_dtypes.float8_e4m3fn, 7), "e5m2": (ml_dtypes.float8_e5m2, 14)}[fmt]
    v = np.moveaxis(np.asarray(x, np.float32).astype(ml_dtypes.bfloat16).astype(np.float64), axis, -1)
    blocks = v.reshape(v.shape[:-1] + (-1, 32))
    amax = np.abs(blocks).max(-1, keepdims=True)
    byte = np.maximum(np.where(amax > 0, np.frexp(amax)[1] - 1 + 127, 0) - down, 1)
    scale = np.exp2(byte - 127.0)
    codes = (blocks / scale).astype(np.float32).astype(dtype).astype(np.float64)
    return np.moveaxis((codes * scale).reshape(v.shape), -1, axis)


WIDE = False


def mx_kscale(k):
    if not WIDE:
        return np.ones(k)
    levels = np.array([10, -10, 5, -5, 0])
    a = np.random.permutation(np.resize(levels, k // 512 * 4)).reshape(k // 512, 4)
    idx = np.arange(k)
    return np.exp2(a[idx // 512, idx % 128 // 32])


BF16 = ml_dtypes.bfloat16


def bf(x):
    return np.asarray(x, np.float32).astype(BF16)


def f64(x):
    return np.asarray(x).astype(np.float64)


B, C, H, W, S = 2, 512, 128, 64, 4
NB = (H // S) * (W // S)
HW = H * W
SS = S * S


def setup_inputs():
    s, t = mx_kscale(C), mx_kscale(C)
    return {"x": bf(np.random.standard_normal((B, C, H, W)) * s[None, :, None, None]),
            "q_blk": bf(np.random.standard_normal((B, NB, C)) * 1.25 * t),
            "k_blk": bf(np.random.standard_normal((B, NB, C)) * 1.25 / t),
            "Wv": bf(np.random.standard_normal((C, C)) / np.sqrt(C) / s[None, :]),
            "bv": bf(np.random.standard_normal(C) * 0.5 / SS)}


def reference(x, q_blk, k_blk, Wv, bv):
    sc = (mxq(f64(q_blk), 2, "e4m3") @ mxq(f64(k_blk), 2, "e4m3").transpose(0, 2, 1)) / np.sqrt(C)
    e = np.exp(sc - sc.max(-1, keepdims=True))
    x_flat = f64(x).reshape(B, C, HW).transpose(0, 2, 1)
    V = (mxq(x_flat, 2, "e4m3") @ mxq(f64(Wv), 1, "e4m3").T) + f64(bv)
    Vsum = V.reshape(B, NB, SS, C).sum(axis=2)
    return (mxq(e, 2, "e4m3") @ mxq(Vsum, 1, "e4m3")) / e.sum(-1, keepdims=True)

@@ -1,0 +1,212 @@
+import math
+from contextlib import ExitStack
+
+import concourse.mybir as mybir
+from concourse.masks import make_identity
+
+F32 = mybir.dt.float32
+BF16 = mybir.dt.bfloat16
+U32 = mybir.dt.uint32
+U8 = mybir.dt.uint8
+FP8X4 = mybir.dt.float8_e4m3fn_x4
+ALU = mybir.AluOpType
+ACT = mybir.ActivationFunctionType
+
+P = 128
+PACK = 4
+BATCH = 2
+C = 512
+PIXELS = 128 * 64
+GROUP = 16
+BLOCKS = PIXELS // GROUP
+TILES = BLOCKS // P
+CHUNK = P * GROUP
+CHUNKS = PIXELS // CHUNK
+RUN = 4
+PIECES = GROUP // RUN
+SCALE = 1.0 / math.sqrt(C)
+
+FLOPS = 2 * BATCH * (PIXELS * C * C + 2 * BLOCKS * BLOCKS * C)
+
+
+def mx_tiles(pool, name, columns):
+    codes = pool.tile([P, columns], U32, name=name + "_codes", align_bytes=64)
+    scales = pool.tile([P, columns], U8, name=name + "_scales", align_bytes=64)
+    return codes, scales
+
+
+def matmul_mx(nc, acc, stationary, moving, columns, start=True, stop=True):
+    nc.tensor.matmul_mx(
+        out=acc,
+        lhsT=stationary[0][:, columns].bitcast(FP8X4),
+        lhsT_scale=stationary[1][:, columns],
+        rhs=moving[0][:].bitcast(FP8X4),
+        rhs_scale=moving[1][:],
+        start=start,
+        stop=stop,
+    )
+
+
+def quantise_rows_along_channels(nc, pools, ident_f32, rows, operand):
+    by_row = pools["load"].tile([P, TILES, C], BF16, name="by_row")
+    nc.sync.dma_start(out=by_row[:], in_=rows.rearrange("(a p) c -> p a c", p=P))
+    words = by_row[:].bitcast(F32).rearrange("p a (q u) -> p a u q", u=2)
+    grouped = pools["grouped"].tile([P, BLOCKS, PACK], BF16, name="grouped_rows", align_bytes=64)
+    grouped_words = grouped[:].bitcast(F32).rearrange("p (h a r) u -> p h a r u", h=2, a=2)
+    for h in range(2):
+        flipped = pools["psum_flip"].tile([P, 2, 2, P], F32, name="flipped")
+        for a in range(2):
+            for u in range(2):
+                nc.tensor.transpose(flipped[:, a, u, :], words[:, 2 * h + a, u, :], ident_f32[:])
+        nc.scalar.copy(out=grouped_words[:, h], in_=flipped[:].rearrange("p a u r -> p a r u"))
+    nc.vector.quantize_mx(
+        out=operand[0][:].bitcast(FP8X4),
+        scales=operand[1][:],
+        in_=grouped[:].rearrange("p r t -> p (r t)"),
+    )
+
+
+def tile_coarseblockattention_pb_kernel(tc, x, q_blk, k_blk, Wv, bv, out):
+    nc = tc.nc
+    with ExitStack() as ctx:
+        pools = {
+            "const": ctx.enter_context(tc.tile_pool(name="const", bufs=1)),
+            "load": ctx.enter_context(tc.tile_pool(name="load", bufs=3)),
+            "grouped": ctx.enter_context(tc.tile_pool(name="grouped", bufs=2)),
+            "raw": ctx.enter_context(tc.tile_pool(name="raw", bufs=4)),
+            "pixels": ctx.enter_context(tc.tile_pool(name="pixels", bufs=2)),
+            "batch": ctx.enter_context(tc.tile_pool(name="batch", bufs=2)),
+            "store": ctx.enter_context(tc.tile_pool(name="store", bufs=4)),
+            "psum_flip": ctx.enter_context(tc.psum_pool(name="psum_flip", bufs=2)),
+            "psum_vsum": ctx.enter_context(tc.psum_pool(name="psum_vsum", bufs=2)),
+            "psum_wide": ctx.enter_context(tc.psum_pool(name="psum_wide", bufs=4)),
+        }
+        const = pools["const"]
+        batch = pools["batch"]
+
+        warm = const.tile([P, 1], F32, name="warm")
+        nc.vector.memset(warm[:], 0.0)
+        nc.scalar.activation(out=warm[:], in_=warm[:], func=ACT.Exp)
+
+        ident_f32 = const.tile([P, P], F32, name="ident_f32")
+        make_identity(nc, ident_f32[:])
+        ident_bf16 = const.tile([P, P], BF16, name="ident_bf16")
+        make_identity(nc, ident_bf16[:])
+
+        wv = mx_tiles(const, "wv", C)
+        quantise_rows_along_channels(nc, pools, ident_f32, Wv, wv)
+
+        bias_bf16 = const.tile([P, C], BF16, name="bias_bf16")
+        nc.scalar.dma_start(out=bias_bf16[:], in_=bv.partition_broadcast(P))
+        group_bias = const.tile([P, C], F32, name="group_bias")
+        nc.vector.tensor_scalar(
+            out=group_bias[:], in0=bias_bf16[:], scalar1=float(GROUP), scalar2=None, op0=ALU.mult
+        )
+
+        x_quads = x.rearrange("b (p t) h w -> b p t (h w)", t=PACK)
+
+        def attention_weights(b):
+            q = mx_tiles(batch, "q", BLOCKS)
+            quantise_rows_along_channels(nc, pools, ident_f32, q_blk[b], q)
+            k = mx_tiles(batch, "k", BLOCKS)
+            quantise_rows_along_channels(nc, pools, ident_f32, k_blk[b], k)
+
+            row_max = batch.tile([P, TILES], F32, name="row_max")
+            score_tiles = []
+            for a in range(TILES):
+                scores = pools["psum_wide"].tile([P, BLOCKS], F32, name="scores", tag="wide")
+                matmul_mx(nc, scores[:], q, k, slice(a * P, (a + 1) * P))
+                nc.vector.tensor_reduce(
+                    out=row_max[:, a : a + 1], in_=scores[:], axis=mybir.AxisListType.X, op=ALU.max
+                )
+                score_tiles.append(scores)
+            exp_bias = batch.tile([P, TILES], F32, name="exp_bias")
+            nc.vector.tensor_scalar(
+                out=exp_bias[:], in0=row_max[:], scalar1=-SCALE, scalar2=None, op0=ALU.mult
+            )
+            row_sum = batch.tile([P, TILES], F32, name="row_sum")
+            e_bf16 = batch.tile([P, TILES, BLOCKS], BF16, name="e_bf16")
+            for a in range(TILES):
+                nc.scalar.activation(
+                    out=e_bf16[:, a, :],
+                    in_=score_tiles[a][:],
+                    func=ACT.Exp,
+                    bias=exp_bias[:, a : a + 1],
+                    scale=SCALE,
+                    accum_out=row_sum[:, a : a + 1],
+                )
+            inv_sum = batch.tile([P, TILES], F32, name="inv_sum")
+            nc.vector.reciprocal(out=inv_sum[:], in_=row_sum[:])
+
+            e_grouped = batch.tile([P, BLOCKS, PACK], BF16, name="e_grouped", align_bytes=64)
+            e_grouped_halves = e_grouped[:].rearrange("p (h a n) t -> p h a n t", h=2, a=2)
+            for h in range(2):
+                e_flipped = pools["psum_flip"].tile([P, 2, PACK, P], BF16, name="e_flipped", tag="flipped")
+                for a in range(2):
+                    for t in range(PACK):
+                        nc.tensor.transpose(
+                            e_flipped[:, a, t, :], e_bf16[:, 2 * h + a, t * P : (t + 1) * P], ident_bf16[:]
+                        )
+                nc.scalar.copy(out=e_grouped_halves[:, h], in_=e_flipped[:].rearrange("p a t n -> p a n t"))
+            e = mx_tiles(batch, "e", BLOCKS)
+            nc.vector.quantize_mx(
+                out=e[0][:].bitcast(FP8X4), scales=e[1][:], in_=e_grouped[:].rearrange("p n t -> p (n t)")
+            )
+            return e, inv_sum
+
+        def group_sums(b):
+            vsum_bf16 = batch.tile([P, CHUNKS, C], BF16, name="vsum_bf16")
+            for t in range(CHUNKS):
+                raw = pools["raw"].tile([P, PACK, CHUNK], BF16, name="raw")
+                nc.sync.dma_start(out=raw[:], in_=x_quads[b, :, :, t * CHUNK : (t + 1) * CHUNK])
+
+                grouped = pools["pixels"].tile([P, GROUP, P, PACK], BF16, name="grouped", align_bytes=64)
+                read = raw[:].rearrange("p t (g s i) -> p s g t i", s=PIECES, i=RUN)
+                write = grouped[:].rearrange("p (s i) g t -> p s g t i", i=RUN)
+                for s in range(PIECES):
+                    if s % 2 == 0:
+                        nc.vector.tensor_copy(out=write[:, s], in_=read[:, s])
+                    else:
+                        nc.scalar.copy(out=write[:, s], in_=read[:, s])
+
+                pixels = mx_tiles(pools["pixels"], "pixels", GROUP * P)
+                for h in range(2):
+                    half = slice(h * GROUP * P // 2, (h + 1) * GROUP * P // 2)
+                    nc.vector.quantize_mx(
+                        out=pixels[0][:, half].bitcast(FP8X4),
+                        scales=pixels[1][:, half],
+                        in_=grouped[:].rearrange("p j g t -> p (j g) t")[:, half, :].rearrange("p c t -> p (c t)"),
+                    )
+
+                vsum = pools["psum_vsum"].tile([P, C], F32, name="vsum")
+                for j in range(GROUP):
+                    matmul_mx(
+                        nc, vsum[:], pixels, wv, slice(j * P, (j + 1) * P), start=(j == 0), stop=(j == GROUP - 1)
+                    )
+                nc.vector.tensor_tensor(out=vsum_bf16[:, t, :], in0=vsum[:], in1=group_bias[:], op=ALU.add)
+
+            vsum_grouped = batch.tile([P, C, PACK], BF16, name="vsum_grouped", align_bytes=64)
+            nc.vector.tensor_copy(out=vsum_grouped[:], in_=vsum_bf16[:].rearrange("p t c -> p c t"))
+            values = mx_tiles(batch, "values", C)
+            nc.vector.quantize_mx(
+                out=values[0][:].bitcast(FP8X4),
+                scales=values[1][:],
+                in_=vsum_grouped[:].rearrange("p c t -> p (c t)"),
+            )
+            return values
+
+        def mix(b, e, inv_sum, values):
+            for a in range(TILES):
+                queries = slice(a * P, (a + 1) * P)
+                mixed = pools["psum_wide"].tile([P, C], F32, name="mixed", tag="wide")
+                matmul_mx(nc, mixed[:], e, values, queries)
+                result = pools["store"].tile([P, C], F32, name="result")
+                nc.scalar.activation(out=result[:], in_=mixed[:], func=ACT.Copy, scale=inv_sum[:, a : a + 1])
+                nc.sync.dma_start(out=out[b, queries, :], in_=result[:])
+
+        e, inv_sum = attention_weights(0)
+        for b in range(BATCH):
+            values = group_sums(b)
+            if b > 0:
+                e, inv_sum = attention_weights(b)
+            mix(b, e, inv_sum, values)

@@ -23,7 +23,10 @@ TILES = BLOCKS // P
 CHUNK = P * GROUP
 CHUNKS = PIXELS // CHUNK
 RUN = 4
-PIECES = GROUP // RUN
+HALF = GROUP // 2
+UNITS_PER_BATCH = 2 * CHUNKS
+UNITS = BATCH * UNITS_PER_BATCH
+RAW_BUFS = 4
 SCALE = 1.0 / math.sqrt(C)
 
 FLOPS = 2 * BATCH * (PIXELS * C * C + 2 * BLOCKS * BLOCKS * C)
@@ -35,7 +38,13 @@ def mx_tiles(pool, name, columns):
     return codes, scales
 
 
-def matmul_mx(nc, acc, stationary, moving, columns, start=True, stop=True):
+def quantise(nc, operand, columns, grouped):
+    nc.vector.quantize_mx(
+        out=operand[0][:, columns].bitcast(FP8X4), scales=operand[1][:, columns], in_=grouped
+    )
+
+
+def matmul_mx(nc, acc, stationary, columns, moving, start=True, stop=True):
     nc.tensor.matmul_mx(
         out=acc,
         lhsT=stationary[0][:, columns].bitcast(FP8X4),
@@ -47,42 +56,201 @@ def matmul_mx(nc, acc, stationary, moving, columns, start=True, stop=True):
     )
 
 
-def quantise_rows_along_channels(nc, pools, ident_f32, rows, operand):
-    by_row = pools["load"].tile([P, TILES, C], BF16, name="by_row")
-    nc.sync.dma_start(out=by_row[:], in_=rows.rearrange("(a p) c -> p a c", p=P))
-    words = by_row[:].bitcast(F32).rearrange("p a (q u) -> p a u q", u=2)
-    grouped = pools["grouped"].tile([P, BLOCKS, PACK], BF16, name="grouped_rows", align_bytes=64)
-    grouped_words = grouped[:].bitcast(F32).rearrange("p (h a r) u -> p h a r u", h=2, a=2)
-    for h in range(2):
-        flipped = pools["psum_flip"].tile([P, 2, 2, P], F32, name="flipped")
-        for a in range(2):
-            for u in range(2):
-                nc.tensor.transpose(flipped[:, a, u, :], words[:, 2 * h + a, u, :], ident_f32[:])
-        nc.scalar.copy(out=grouped_words[:, h], in_=flipped[:].rearrange("p a u r -> p a r u"))
-    nc.vector.quantize_mx(
-        out=operand[0][:].bitcast(FP8X4),
-        scales=operand[1][:],
-        in_=grouped[:].rearrange("p r t -> p (r t)"),
-    )
-
-
 def tile_coarseblockattention_pb_kernel(tc, x, q_blk, k_blk, Wv, bv, out):
     nc = tc.nc
     with ExitStack() as ctx:
-        pools = {
-            "const": ctx.enter_context(tc.tile_pool(name="const", bufs=1)),
-            "load": ctx.enter_context(tc.tile_pool(name="load", bufs=3)),
-            "grouped": ctx.enter_context(tc.tile_pool(name="grouped", bufs=2)),
-            "raw": ctx.enter_context(tc.tile_pool(name="raw", bufs=4)),
-            "pixels": ctx.enter_context(tc.tile_pool(name="pixels", bufs=2)),
-            "batch": ctx.enter_context(tc.tile_pool(name="batch", bufs=2)),
-            "store": ctx.enter_context(tc.tile_pool(name="store", bufs=4)),
-            "psum_flip": ctx.enter_context(tc.psum_pool(name="psum_flip", bufs=2)),
-            "psum_vsum": ctx.enter_context(tc.psum_pool(name="psum_vsum", bufs=2)),
-            "psum_wide": ctx.enter_context(tc.psum_pool(name="psum_wide", bufs=4)),
-        }
-        const = pools["const"]
-        batch = pools["batch"]
+        const = ctx.enter_context(tc.tile_pool(name="const", bufs=1))
+        rows_pool = ctx.enter_context(tc.tile_pool(name="rows", bufs=1 + 2 * BATCH))
+        raw_pool = ctx.enter_context(tc.tile_pool(name="raw", bufs=RAW_BUFS))
+        pixel_pool = ctx.enter_context(tc.tile_pool(name="pixels", bufs=2))
+        batch_pool = ctx.enter_context(tc.tile_pool(name="batch", bufs=BATCH))
+        store_pool = ctx.enter_context(tc.tile_pool(name="store", bufs=4))
+        psum_flip = ctx.enter_context(tc.psum_pool(name="psum_flip", bufs=2))
+        psum_vsum = ctx.enter_context(tc.psum_pool(name="psum_vsum", bufs=2))
+        psum_scores = ctx.enter_context(tc.psum_pool(name="psum_scores", bufs=2))
+        psum_mixed = ctx.enter_context(tc.psum_pool(name="psum_mixed", bufs=2))
+        ctx.enter_context(tc.manual_schedule())
+
+        all_columns = slice(0, BLOCKS)
+        x_quads = x.rearrange("b (p t) h w -> b p t (h w)", t=PACK)
+
+        def load_rows(rows):
+            by_row = rows_pool.tile([P, TILES, C], BF16, name="by_row")
+            nc.sync.dma_start(out=by_row[:], in_=rows.rearrange("(a p) c -> p a c", p=P))
+            return by_row
+
+        raw = {}
+
+        def load_chunk(c):
+            b, t = divmod(c, CHUNKS)
+            raw[c] = raw_pool.tile([P, PACK, CHUNK], BF16, name="raw")
+            nc.sync.dma_start(out=raw[c][:], in_=x_quads[b, :, :, t * CHUNK : (t + 1) * CHUNK])
+
+        def flip_rows(by_row, grouped):
+            words = by_row[:].bitcast(F32).rearrange("p a (q u) -> p a u q", u=2)
+            grouped_words = grouped[:].bitcast(F32).rearrange("p (h a r) u -> p h a r u", h=2, a=2)
+            for h in range(2):
+                flipped = psum_flip.tile([P, 2, 2, P], F32, name="flipped")
+                for a in range(2):
+                    for u in range(2):
+                        nc.tensor.transpose(flipped[:, a, u, :], words[:, 2 * h + a, u, :], ident_f32[:])
+                nc.scalar.copy(out=grouped_words[:, h], in_=flipped[:].rearrange("p a u r -> p a r u"))
+
+        grouped = {}
+        pixels = {}
+        vsum = {}
+        vsum_bf16 = {}
+
+        def regroup(unit):
+            c, h = divmod(unit, 2)
+            if h == 0:
+                grouped[c] = pixel_pool.tile([P, GROUP, P, PACK], BF16, name="grouped", align_bytes=64)
+            read = raw[c][:].rearrange("p t (g s i) -> p s g t i", s=GROUP // RUN, i=RUN)
+            write = grouped[c][:].rearrange("p (s i) g t -> p s g t i", i=RUN)
+            nc.vector.tensor_copy(out=write[:, 2 * h], in_=read[:, 2 * h])
+            nc.scalar.copy(out=write[:, 2 * h + 1], in_=read[:, 2 * h + 1])
+
+        def project(unit):
+            c, h = divmod(unit, 2)
+            if h == 0:
+                pixels[c] = mx_tiles(pixel_pool, "pixels", GROUP * P)
+                vsum[c] = psum_vsum.tile([P, C], F32, name="vsum")
+            planes = slice(h * HALF, (h + 1) * HALF)
+            quantise(
+                nc,
+                pixels[c],
+                slice(h * HALF * P, (h + 1) * HALF * P),
+                grouped[c][:, planes, :, :].rearrange("p j g t -> p (j g t)"),
+            )
+            for j in range(h * HALF, (h + 1) * HALF):
+                matmul_mx(
+                    nc, vsum[c][:], pixels[c], slice(j * P, (j + 1) * P), wv, start=(j == 0), stop=(j == GROUP - 1)
+                )
+
+        def leave(c):
+            b, t = divmod(c, CHUNKS)
+            nc.vector.tensor_tensor(out=vsum_bf16[b][:, t, :], in0=vsum[c][:], in1=group_bias[:], op=ALU.add)
+
+        def side_stages(b, q_rows, k_rows):
+            q = mx_tiles(batch_pool, "q", BLOCKS)
+            k = mx_tiles(batch_pool, "k", BLOCKS)
+            e = mx_tiles(batch_pool, "e", BLOCKS)
+            values = mx_tiles(batch_pool, "values", C)
+            q_grouped = batch_pool.tile([P, BLOCKS, PACK], BF16, name="q_grouped", align_bytes=64)
+            k_grouped = batch_pool.tile([P, BLOCKS, PACK], BF16, name="k_grouped", align_bytes=64)
+            e_grouped = batch_pool.tile([P, BLOCKS, PACK], BF16, name="e_grouped", align_bytes=64)
+            vsum_grouped = batch_pool.tile([P, C, PACK], BF16, name="vsum_grouped", align_bytes=64)
+            row_max = batch_pool.tile([P, TILES], F32, name="row_max")
+            exp_bias = batch_pool.tile([P, TILES], F32, name="exp_bias")
+            row_sum = batch_pool.tile([P, TILES], F32, name="row_sum")
+            inv_sum = batch_pool.tile([P, TILES], F32, name="inv_sum")
+            e_bf16 = batch_pool.tile([P, TILES, BLOCKS], BF16, name="e_bf16")
+            vsum_bf16[b] = batch_pool.tile([P, CHUNKS, C], BF16, name="vsum_bf16")
+            scores = {}
+
+            def score(h):
+                for a in (2 * h, 2 * h + 1):
+                    scores[a] = psum_scores.tile([P, BLOCKS], F32, name="scores")
+                    matmul_mx(nc, scores[a][:], q, slice(a * P, (a + 1) * P), k)
+
+            def maxima(h):
+                for a in (2 * h, 2 * h + 1):
+                    nc.vector.tensor_reduce(
+                        out=row_max[:, a : a + 1], in_=scores[a][:], axis=mybir.AxisListType.X, op=ALU.max
+                    )
+                pair = slice(2 * h, 2 * h + 2)
+                nc.vector.tensor_scalar(
+                    out=exp_bias[:, pair], in0=row_max[:, pair], scalar1=-SCALE, scalar2=None, op0=ALU.mult
+                )
+
+            def exponentials(h):
+                for a in (2 * h, 2 * h + 1):
+                    nc.scalar.activation(
+                        out=e_bf16[:, a, :],
+                        in_=scores[a][:],
+                        func=ACT.Exp,
+                        bias=exp_bias[:, a : a + 1],
+                        scale=SCALE,
+                        accum_out=row_sum[:, a : a + 1],
+                    )
+
+            def flip_e(h):
+                e_flipped = psum_flip.tile([P, 2, PACK, P], BF16, name="e_flipped", tag="flipped")
+                for a in range(2):
+                    for t in range(PACK):
+                        nc.tensor.transpose(
+                            e_flipped[:, a, t, :], e_bf16[:, 2 * h + a, t * P : (t + 1) * P], ident_bf16[:]
+                        )
+                nc.scalar.copy(
+                    out=e_grouped[:].rearrange("p (h a n) t -> p h a n t", h=2, a=2)[:, h],
+                    in_=e_flipped[:].rearrange("p a t n -> p a n t"),
+                )
+
+            def mix(h):
+                for a in (2 * h, 2 * h + 1):
+                    queries = slice(a * P, (a + 1) * P)
+                    mixed = psum_mixed.tile([P, C], F32, name="mixed")
+                    matmul_mx(nc, mixed[:], e, queries, values)
+                    result = store_pool.tile([P, C], F32, name="result")
+                    nc.scalar.activation(out=result[:], in_=mixed[:], func=ACT.Copy, scale=inv_sum[:, a : a + 1])
+                    nc.sync.dma_start(out=out[b, queries, :], in_=result[:])
+
+            def stage_0():
+                flip_rows(q_rows, q_grouped)
+
+            def stage_1():
+                quantise(nc, q, all_columns, q_grouped[:].rearrange("p r t -> p (r t)"))
+                flip_rows(k_rows, k_grouped)
+
+            def stage_2():
+                quantise(nc, k, all_columns, k_grouped[:].rearrange("p r t -> p (r t)"))
+                score(0)
+
+            def stage_3():
+                maxima(0)
+
+            def stage_4():
+                exponentials(0)
+
+            def stage_5():
+                score(1)
+
+            def stage_6():
+                maxima(1)
+                flip_e(0)
+
+            def stage_7():
+                exponentials(1)
+
+            def stage_8():
+                flip_e(1)
+
+            def stage_9():
+                quantise(nc, e, all_columns, e_grouped[:].rearrange("p n t -> p (n t)"))
+                nc.vector.reciprocal(out=inv_sum[:], in_=row_sum[:])
+
+            def stage_10():
+                nc.vector.tensor_copy(out=vsum_grouped[:], in_=vsum_bf16[b][:].rearrange("p t c -> p c t"))
+
+            def stage_11():
+                quantise(nc, values, all_columns, vsum_grouped[:].rearrange("p c t -> p (c t)"))
+                mix(0)
+
+            def stage_12():
+                mix(1)
+
+            return [
+                stage_0, stage_1, stage_2, stage_3, stage_4, stage_5, stage_6,
+                stage_7, stage_8, stage_9, stage_10, stage_11, stage_12,
+            ]
+
+        bias_bf16 = const.tile([P, C], BF16, name="bias_bf16")
+        nc.scalar.dma_start(out=bias_bf16[:], in_=bv.partition_broadcast(P))
+        wv_rows = load_rows(Wv)
+        load_chunk(0)
+        first_rows = (load_rows(q_blk[0]), load_rows(k_blk[0]))
+        for c in range(1, RAW_BUFS):
+            load_chunk(c)
 
         warm = const.tile([P, 1], F32, name="warm")
         nc.vector.memset(warm[:], 0.0)
@@ -94,119 +262,28 @@ def tile_coarseblockattention_pb_kernel(tc, x, q_blk, k_blk, Wv, bv, out):
         make_identity(nc, ident_bf16[:])
 
         wv = mx_tiles(const, "wv", C)
-        quantise_rows_along_channels(nc, pools, ident_f32, Wv, wv)
+        wv_grouped = const.tile([P, C, PACK], BF16, name="wv_grouped", align_bytes=64)
+        flip_rows(wv_rows, wv_grouped)
+        quantise(nc, wv, all_columns, wv_grouped[:].rearrange("p r t -> p (r t)"))
 
-        bias_bf16 = const.tile([P, C], BF16, name="bias_bf16")
-        nc.scalar.dma_start(out=bias_bf16[:], in_=bv.partition_broadcast(P))
         group_bias = const.tile([P, C], F32, name="group_bias")
         nc.vector.tensor_scalar(
             out=group_bias[:], in0=bias_bf16[:], scalar1=float(GROUP), scalar2=None, op0=ALU.mult
         )
 
-        x_quads = x.rearrange("b (p t) h w -> b p t (h w)", t=PACK)
+        side = [side_stages(0, first_rows[0], first_rows[1])]
+        side.append(side_stages(1, load_rows(q_blk[1]), load_rows(k_blk[1])))
 
-        def attention_weights(b):
-            q = mx_tiles(batch, "q", BLOCKS)
-            quantise_rows_along_channels(nc, pools, ident_f32, q_blk[b], q)
-            k = mx_tiles(batch, "k", BLOCKS)
-            quantise_rows_along_channels(nc, pools, ident_f32, k_blk[b], k)
-
-            row_max = batch.tile([P, TILES], F32, name="row_max")
-            score_tiles = []
-            for a in range(TILES):
-                scores = pools["psum_wide"].tile([P, BLOCKS], F32, name="scores", tag="wide")
-                matmul_mx(nc, scores[:], q, k, slice(a * P, (a + 1) * P))
-                nc.vector.tensor_reduce(
-                    out=row_max[:, a : a + 1], in_=scores[:], axis=mybir.AxisListType.X, op=ALU.max
-                )
-                score_tiles.append(scores)
-            exp_bias = batch.tile([P, TILES], F32, name="exp_bias")
-            nc.vector.tensor_scalar(
-                out=exp_bias[:], in0=row_max[:], scalar1=-SCALE, scalar2=None, op0=ALU.mult
-            )
-            row_sum = batch.tile([P, TILES], F32, name="row_sum")
-            e_bf16 = batch.tile([P, TILES, BLOCKS], BF16, name="e_bf16")
-            for a in range(TILES):
-                nc.scalar.activation(
-                    out=e_bf16[:, a, :],
-                    in_=score_tiles[a][:],
-                    func=ACT.Exp,
-                    bias=exp_bias[:, a : a + 1],
-                    scale=SCALE,
-                    accum_out=row_sum[:, a : a + 1],
-                )
-            inv_sum = batch.tile([P, TILES], F32, name="inv_sum")
-            nc.vector.reciprocal(out=inv_sum[:], in_=row_sum[:])
-
-            e_grouped = batch.tile([P, BLOCKS, PACK], BF16, name="e_grouped", align_bytes=64)
-            e_grouped_halves = e_grouped[:].rearrange("p (h a n) t -> p h a n t", h=2, a=2)
-            for h in range(2):
-                e_flipped = pools["psum_flip"].tile([P, 2, PACK, P], BF16, name="e_flipped", tag="flipped")
-                for a in range(2):
-                    for t in range(PACK):
-                        nc.tensor.transpose(
-                            e_flipped[:, a, t, :], e_bf16[:, 2 * h + a, t * P : (t + 1) * P], ident_bf16[:]
-                        )
-                nc.scalar.copy(out=e_grouped_halves[:, h], in_=e_flipped[:].rearrange("p a t n -> p a n t"))
-            e = mx_tiles(batch, "e", BLOCKS)
-            nc.vector.quantize_mx(
-                out=e[0][:].bitcast(FP8X4), scales=e[1][:], in_=e_grouped[:].rearrange("p n t -> p (n t)")
-            )
-            return e, inv_sum
-
-        def group_sums(b):
-            vsum_bf16 = batch.tile([P, CHUNKS, C], BF16, name="vsum_bf16")
-            for t in range(CHUNKS):
-                raw = pools["raw"].tile([P, PACK, CHUNK], BF16, name="raw")
-                nc.sync.dma_start(out=raw[:], in_=x_quads[b, :, :, t * CHUNK : (t + 1) * CHUNK])
-
-                grouped = pools["pixels"].tile([P, GROUP, P, PACK], BF16, name="grouped", align_bytes=64)
-                read = raw[:].rearrange("p t (g s i) -> p s g t i", s=PIECES, i=RUN)
-                write = grouped[:].rearrange("p (s i) g t -> p s g t i", i=RUN)
-                for s in range(PIECES):
-                    if s % 2 == 0:
-                        nc.vector.tensor_copy(out=write[:, s], in_=read[:, s])
-                    else:
-                        nc.scalar.copy(out=write[:, s], in_=read[:, s])
-
-                pixels = mx_tiles(pools["pixels"], "pixels", GROUP * P)
-                for h in range(2):
-                    half = slice(h * GROUP * P // 2, (h + 1) * GROUP * P // 2)
-                    nc.vector.quantize_mx(
-                        out=pixels[0][:, half].bitcast(FP8X4),
-                        scales=pixels[1][:, half],
-                        in_=grouped[:].rearrange("p j g t -> p (j g) t")[:, half, :].rearrange("p c t -> p (c t)"),
-                    )
-
-                vsum = pools["psum_vsum"].tile([P, C], F32, name="vsum")
-                for j in range(GROUP):
-                    matmul_mx(
-                        nc, vsum[:], pixels, wv, slice(j * P, (j + 1) * P), start=(j == 0), stop=(j == GROUP - 1)
-                    )
-                nc.vector.tensor_tensor(out=vsum_bf16[:, t, :], in0=vsum[:], in1=group_bias[:], op=ALU.add)
-
-            vsum_grouped = batch.tile([P, C, PACK], BF16, name="vsum_grouped", align_bytes=64)
-            nc.vector.tensor_copy(out=vsum_grouped[:], in_=vsum_bf16[:].rearrange("p t c -> p c t"))
-            values = mx_tiles(batch, "values", C)
-            nc.vector.quantize_mx(
-                out=values[0][:].bitcast(FP8X4),
-                scales=values[1][:],
-                in_=vsum_grouped[:].rearrange("p c t -> p (c t)"),
-            )
-            return values
-
-        def mix(b, e, inv_sum, values):
-            for a in range(TILES):
-                queries = slice(a * P, (a + 1) * P)
-                mixed = pools["psum_wide"].tile([P, C], F32, name="mixed", tag="wide")
-                matmul_mx(nc, mixed[:], e, values, queries)
-                result = pools["store"].tile([P, C], F32, name="result")
-                nc.scalar.activation(out=result[:], in_=mixed[:], func=ACT.Copy, scale=inv_sum[:, a : a + 1])
-                nc.sync.dma_start(out=out[b, queries, :], in_=result[:])
-
-        e, inv_sum = attention_weights(0)
-        for b in range(BATCH):
-            values = group_sums(b)
-            if b > 0:
-                e, inv_sum = attention_weights(b)
-            mix(b, e, inv_sum, values)
+        for i in range(UNITS_PER_BATCH * (BATCH - 1) + len(side[0])):
+            if i < UNITS:
+                regroup(i)
+                if i % 2 == 1 and i // 2 + RAW_BUFS < BATCH * CHUNKS:
+                    load_chunk(i // 2 + RAW_BUFS)
+            for b in range(BATCH):
+                stage = i - b * UNITS_PER_BATCH
+                if 0 <= stage < len(side[b]):
+                    side[b][stage]()
+            if 1 <= i <= UNITS:
+                project(i - 1)
+            if i % 2 == 1 and 0 <= (i - 3) // 2 < BATCH * CHUNKS:
+                leave((i - 3) // 2)

@@ -69,7 +69,6 @@ def tile_coarseblockattention_pb_kernel(tc, x, q_blk, k_blk, Wv, bv, out):
         psum_vsum = ctx.enter_context(tc.psum_pool(name="psum_vsum", bufs=2))
         psum_scores = ctx.enter_context(tc.psum_pool(name="psum_scores", bufs=2))
         psum_mixed = ctx.enter_context(tc.psum_pool(name="psum_mixed", bufs=2))
-        ctx.enter_context(tc.manual_schedule())
 
         all_columns = slice(0, BLOCKS)
         x_quads = x.rearrange("b (p t) h w -> b p t (h w)", t=PACK)

@@ -114,17 +114,17 @@ def tile_coarseblockattention_pb_kernel(tc, x, q_blk, k_blk, Wv, bv, out):
             if h == 0:
                 pixels[c] = mx_tiles(pixel_pool, "pixels", GROUP * P)
                 vsum[c] = psum_vsum.tile([P, C], F32, name="vsum")
-            planes = slice(h * HALF, (h + 1) * HALF)
-            quantise(
-                nc,
-                pixels[c],
-                slice(h * HALF * P, (h + 1) * HALF * P),
-                grouped[c][:, planes, :, :].rearrange("p j g t -> p (j g t)"),
-            )
-            for j in range(h * HALF, (h + 1) * HALF):
-                matmul_mx(
-                    nc, vsum[c][:], pixels[c], slice(j * P, (j + 1) * P), wv, start=(j == 0), stop=(j == GROUP - 1)
+            for s in (2 * h, 2 * h + 1):
+                quantise(
+                    nc,
+                    pixels[c],
+                    slice(s * RUN * P, (s + 1) * RUN * P),
+                    grouped[c][:, s * RUN : (s + 1) * RUN, :, :].rearrange("p j g t -> p (j g t)"),
                 )
+                for j in range(s * RUN, (s + 1) * RUN):
+                    matmul_mx(
+                        nc, vsum[c][:], pixels[c], slice(j * P, (j + 1) * P), wv, start=(j == 0), stop=(j == GROUP - 1)
+                    )
 
         def leave(c):
             b, t = divmod(c, CHUNKS)
@@ -191,7 +191,12 @@ def tile_coarseblockattention_pb_kernel(tc, x, q_blk, k_blk, Wv, bv, out):
                     mixed = psum_mixed.tile([P, C], F32, name="mixed")
                     matmul_mx(nc, mixed[:], e, queries, values)
                     result = store_pool.tile([P, C], F32, name="result")
-                    nc.scalar.activation(out=result[:], in_=mixed[:], func=ACT.Copy, scale=inv_sum[:, a : a + 1])
+                    if a % 2 == 0:
+                        nc.scalar.activation(out=result[:], in_=mixed[:], func=ACT.Copy, scale=inv_sum[:, a : a + 1])
+                    else:
+                        nc.vector.tensor_scalar(
+                            out=result[:], in0=mixed[:], scalar1=inv_sum[:, a : a + 1], scalar2=None, op0=ALU.mult
+                        )
                     nc.sync.dma_start(out=out[b, queries, :], in_=result[:])
 
             def stage_0():

@@ -248,8 +248,11 @@ def tile_coarseblockattention_pb_kernel(tc, x, q_blk, k_blk, Wv, bv, out):
                 stage_7, stage_8, stage_9, stage_10, stage_11, stage_12,
             ]
 
-        bias_bf16 = const.tile([P, C], BF16, name="bias_bf16")
-        nc.scalar.dma_start(out=bias_bf16[:], in_=bv.partition_broadcast(P))
+        bias_row = const.tile([P, C], BF16, name="bias_row")
+        nc.vector.memset(bias_row[:], 0.0)
+        nc.scalar.dma_start(out=bias_row[0:1, :], in_=bv.unsqueeze(0))
+        group_weights = const.tile([P, P], BF16, name="group_weights")
+        nc.vector.memset(group_weights[:], float(GROUP))
         wv_rows = load_rows(Wv)
         load_chunk(0)
         first_rows = (load_rows(q_blk[0]), load_rows(k_blk[0]))
@@ -271,9 +274,9 @@ def tile_coarseblockattention_pb_kernel(tc, x, q_blk, k_blk, Wv, bv, out):
         quantise(nc, wv, all_columns, wv_grouped[:].rearrange("p r t -> p (r t)"))
 
         group_bias = const.tile([P, C], F32, name="group_bias")
-        nc.vector.tensor_scalar(
-            out=group_bias[:], in0=bias_bf16[:], scalar1=float(GROUP), scalar2=None, op0=ALU.mult
-        )
+        spread = psum_mixed.tile([P, C], F32, name="spread", tag="mixed")
+        nc.tensor.matmul(spread[:], lhsT=group_weights[:], rhs=bias_row[:], start=True, stop=True)
+        nc.vector.tensor_copy(out=group_bias[:], in_=spread[:])
 
         side = [side_stages(0, first_rows[0], first_rows[1])]
         side.append(side_stages(1, load_rows(q_blk[1]), load_rows(k_blk[1])))

@@ -26,6 +26,8 @@ RUN = 4
 HALF = GROUP // 2
 UNITS_PER_BATCH = 2 * CHUNKS
 UNITS = BATCH * UNITS_PER_BATCH
+VECTOR_GROUPS = 112
+LAST_SCALAR_GROUPS = 96
 RAW_BUFS = 4
 SCALE = 1.0 / math.sqrt(C)
 
@@ -67,9 +69,9 @@ def tile_coarseblockattention_pb_kernel(tc, x, q_blk, k_blk, Wv, bv, out):
         store_pool = ctx.enter_context(tc.tile_pool(name="store", bufs=4))
         psum_flip = ctx.enter_context(tc.psum_pool(name="psum_flip", bufs=2))
         psum_vsum = ctx.enter_context(tc.psum_pool(name="psum_vsum", bufs=2))
-        psum_scores = ctx.enter_context(tc.psum_pool(name="psum_scores", bufs=2))
-        psum_mixed = ctx.enter_context(tc.psum_pool(name="psum_mixed", bufs=2))
+        psum_wide = ctx.enter_context(tc.psum_pool(name="psum_wide", bufs=TILES))
 
+        ctx.enter_context(tc.manual_schedule())
         all_columns = slice(0, BLOCKS)
         x_quads = x.rearrange("b (p t) h w -> b p t (h w)", t=PACK)
 
@@ -80,20 +82,34 @@ def tile_coarseblockattention_pb_kernel(tc, x, q_blk, k_blk, Wv, bv, out):
 
         raw = {}
 
-        def load_chunk(c):
+        def load_chunk(c, piece=0, pieces=1):
             b, t = divmod(c, CHUNKS)
-            raw[c] = raw_pool.tile([P, PACK, CHUNK], BF16, name="raw")
-            nc.sync.dma_start(out=raw[c][:], in_=x_quads[b, :, :, t * CHUNK : (t + 1) * CHUNK])
+            if piece == 0:
+                raw[c] = raw_pool.tile([P, PACK, CHUNK], BF16, name="raw")
+            width = CHUNK // pieces
+            a = piece * width
+            nc.sync.dma_start(
+                out=raw[c][:, :, a : a + width], in_=x_quads[b, :, :, t * CHUNK + a : t * CHUNK + a + width]
+            )
 
-        def flip_rows(by_row, grouped):
+        def flip_half(words, grouped, copy, pattern="p a u r -> p a r u"):
+            flipped = psum_flip.tile([P, 2, 2, P], F32, name="flipped")
+            for a in range(2):
+                for u in range(2):
+                    nc.tensor.transpose(flipped[:, a, u, :], words[:, a, u, :], ident_f32[:])
+            copy(out=grouped, in_=flipped[:].rearrange(pattern))
+
+        def flip_rows(by_row, grouped, copies):
             words = by_row[:].bitcast(F32).rearrange("p a (q u) -> p a u q", u=2)
             grouped_words = grouped[:].bitcast(F32).rearrange("p (h a r) u -> p h a r u", h=2, a=2)
             for h in range(2):
-                flipped = psum_flip.tile([P, 2, 2, P], F32, name="flipped")
-                for a in range(2):
-                    for u in range(2):
-                        nc.tensor.transpose(flipped[:, a, u, :], words[:, 2 * h + a, u, :], ident_f32[:])
-                nc.scalar.copy(out=grouped_words[:, h], in_=flipped[:].rearrange("p a u r -> p a r u"))
+                flip_half(words[:, 2 * h : 2 * h + 2], grouped_words[:, h], copies[h])
+
+        def flip_keys(by_row, grouped, copies):
+            words = by_row[:].bitcast(F32).rearrange("p a (q u) -> p a u q", u=2)
+            grouped_words = grouped[:].bitcast(F32).rearrange("p (h r a) u -> p h r a u", h=2, a=2)
+            for h in range(2):
+                flip_half(words[:, 2 * h : 2 * h + 2], grouped_words[:, h], copies[h], "p a u r -> p r a u")
 
         grouped = {}
         pixels = {}
@@ -106,8 +122,24 @@ def tile_coarseblockattention_pb_kernel(tc, x, q_blk, k_blk, Wv, bv, out):
                 grouped[c] = pixel_pool.tile([P, GROUP, P, PACK], BF16, name="grouped", align_bytes=64)
             read = raw[c][:].rearrange("p t (g s i) -> p s g t i", s=GROUP // RUN, i=RUN)
             write = grouped[c][:].rearrange("p (s i) g t -> p s g t i", i=RUN)
-            nc.vector.tensor_copy(out=write[:, 2 * h], in_=read[:, 2 * h])
-            nc.scalar.copy(out=write[:, 2 * h + 1], in_=read[:, 2 * h + 1])
+
+            def copy(engine_copy, s, groups):
+                engine_copy(out=write[:, s, groups], in_=read[:, s, groups])
+
+            if c < 1:
+                groups = slice(h * P // 2, (h + 1) * P // 2)
+                for s in (0, 1):
+                    copy(nc.vector.tensor_copy, s, groups)
+                    copy(nc.scalar.copy, s + 2, groups)
+                return
+            if unit == UNITS - 1:
+                copy(nc.vector.tensor_copy, 2 * h, slice(0, P))
+                copy(nc.scalar.copy, 2 * h + 1, slice(0, LAST_SCALAR_GROUPS))
+                copy(nc.vector.tensor_copy, 2 * h + 1, slice(LAST_SCALAR_GROUPS, P))
+                return
+            copy(nc.vector.tensor_copy, 2 * h, slice(0, VECTOR_GROUPS))
+            copy(nc.scalar.copy, 2 * h + 1, slice(0, P))
+            copy(nc.scalar.copy, 2 * h, slice(VECTOR_GROUPS, P))
 
         def project(unit):
             c, h = divmod(unit, 2)
@@ -130,7 +162,7 @@ def tile_coarseblockattention_pb_kernel(tc, x, q_blk, k_blk, Wv, bv, out):
             b, t = divmod(c, CHUNKS)
             nc.vector.tensor_tensor(out=vsum_bf16[b][:, t, :], in0=vsum[c][:], in1=group_bias[:], op=ALU.add)
 
-        def side_stages(b, q_rows, k_rows):
+        def side_stages(b, q_rows, k_rows, copies):
             q = mx_tiles(batch_pool, "q", BLOCKS)
             k = mx_tiles(batch_pool, "k", BLOCKS)
             e = mx_tiles(batch_pool, "e", BLOCKS)
@@ -147,9 +179,9 @@ def tile_coarseblockattention_pb_kernel(tc, x, q_blk, k_blk, Wv, bv, out):
             vsum_bf16[b] = batch_pool.tile([P, CHUNKS, C], BF16, name="vsum_bf16")
             scores = {}
 
-            def score(h):
-                for a in (2 * h, 2 * h + 1):
-                    scores[a] = psum_scores.tile([P, BLOCKS], F32, name="scores")
+            def score():
+                for a in range(TILES):
+                    scores[a] = psum_wide.tile([P, BLOCKS], F32, name="scores", tag="wide")
                     matmul_mx(nc, scores[a][:], q, slice(a * P, (a + 1) * P), k)
 
             def maxima(h):
@@ -174,21 +206,14 @@ def tile_coarseblockattention_pb_kernel(tc, x, q_blk, k_blk, Wv, bv, out):
                     )
 
             def flip_e(h):
-                e_flipped = psum_flip.tile([P, 2, PACK, P], BF16, name="e_flipped", tag="flipped")
-                for a in range(2):
-                    for t in range(PACK):
-                        nc.tensor.transpose(
-                            e_flipped[:, a, t, :], e_bf16[:, 2 * h + a, t * P : (t + 1) * P], ident_bf16[:]
-                        )
-                nc.scalar.copy(
-                    out=e_grouped[:].rearrange("p (h a n) t -> p h a n t", h=2, a=2)[:, h],
-                    in_=e_flipped[:].rearrange("p a t n -> p a n t"),
-                )
+                words = e_bf16[:].bitcast(F32).rearrange("p a (u q) -> p a u q", u=2)
+                grouped_words = e_grouped[:].bitcast(F32).rearrange("p (h a r) u -> p h a r u", h=2, a=2)
+                flip_half(words[:, 2 * h : 2 * h + 2], grouped_words[:, h], nc.scalar.copy)
 
-            def mix(h):
-                for a in (2 * h, 2 * h + 1):
+            def mix():
+                for a in range(TILES):
                     queries = slice(a * P, (a + 1) * P)
-                    mixed = psum_mixed.tile([P, C], F32, name="mixed")
+                    mixed = psum_wide.tile([P, C], F32, name="mixed", tag="wide")
                     matmul_mx(nc, mixed[:], e, queries, values)
                     result = store_pool.tile([P, C], F32, name="result")
                     if a % 2 == 0:
@@ -199,64 +224,46 @@ def tile_coarseblockattention_pb_kernel(tc, x, q_blk, k_blk, Wv, bv, out):
                         )
                     nc.sync.dma_start(out=out[b, queries, :], in_=result[:])
 
-            def stage_0():
-                flip_rows(q_rows, q_grouped)
+            def flip_q():
+                flip_rows(q_rows, q_grouped, copies)
 
-            def stage_1():
+            def flip_k():
                 quantise(nc, q, all_columns, q_grouped[:].rearrange("p r t -> p (r t)"))
-                flip_rows(k_rows, k_grouped)
+                flip_keys(k_rows, k_grouped, copies)
 
-            def stage_2():
+            def quantise_k():
                 quantise(nc, k, all_columns, k_grouped[:].rearrange("p r t -> p (r t)"))
-                score(0)
 
-            def stage_3():
-                maxima(0)
-
-            def stage_4():
-                exponentials(0)
-
-            def stage_5():
-                score(1)
-
-            def stage_6():
-                maxima(1)
-                flip_e(0)
-
-            def stage_7():
-                exponentials(1)
-
-            def stage_8():
-                flip_e(1)
-
-            def stage_9():
+            def finish_e():
                 quantise(nc, e, all_columns, e_grouped[:].rearrange("p n t -> p (n t)"))
                 nc.vector.reciprocal(out=inv_sum[:], in_=row_sum[:])
 
-            def stage_10():
+            def group_values():
                 nc.vector.tensor_copy(out=vsum_grouped[:], in_=vsum_bf16[b][:].rearrange("p t c -> p c t"))
 
-            def stage_11():
+            def output():
                 quantise(nc, values, all_columns, vsum_grouped[:].rearrange("p c t -> p (c t)"))
-                mix(0)
-
-            def stage_12():
-                mix(1)
+                mix()
 
             return [
-                stage_0, stage_1, stage_2, stage_3, stage_4, stage_5, stage_6,
-                stage_7, stage_8, stage_9, stage_10, stage_11, stage_12,
+                flip_q, flip_k, quantise_k, score,
+                lambda: maxima(0), lambda: maxima(1),
+                lambda: exponentials(0), lambda: exponentials(1),
+                lambda: flip_e(0), lambda: flip_e(1),
+                finish_e, group_values, output,
             ]
 
         bias_row = const.tile([P, C], BF16, name="bias_row")
         nc.vector.memset(bias_row[:], 0.0)
-        nc.scalar.dma_start(out=bias_row[0:1, :], in_=bv.unsqueeze(0))
+        nc.sync.dma_start(out=bias_row[0:1, :], in_=bv.unsqueeze(0))
         group_weights = const.tile([P, P], BF16, name="group_weights")
         nc.vector.memset(group_weights[:], float(GROUP))
-        wv_rows = load_rows(Wv)
-        load_chunk(0)
         first_rows = (load_rows(q_blk[0]), load_rows(k_blk[0]))
-        for c in range(1, RAW_BUFS):
+        wv_rows = load_rows(Wv)
+        for c in range(2):
+            for piece in range(2):
+                load_chunk(c, piece, 2)
+        for c in range(2, RAW_BUFS):
             load_chunk(c)
 
         warm = const.tile([P, 1], F32, name="warm")
@@ -265,32 +272,63 @@ def tile_coarseblockattention_pb_kernel(tc, x, q_blk, k_blk, Wv, bv, out):
 
         ident_f32 = const.tile([P, P], F32, name="ident_f32")
         make_identity(nc, ident_f32[:])
-        ident_bf16 = const.tile([P, P], BF16, name="ident_bf16")
-        make_identity(nc, ident_bf16[:])
 
         wv = mx_tiles(const, "wv", C)
         wv_grouped = const.tile([P, C, PACK], BF16, name="wv_grouped", align_bytes=64)
-        flip_rows(wv_rows, wv_grouped)
-        quantise(nc, wv, all_columns, wv_grouped[:].rearrange("p r t -> p (r t)"))
 
         group_bias = const.tile([P, C], F32, name="group_bias")
-        spread = psum_mixed.tile([P, C], F32, name="spread", tag="mixed")
-        nc.tensor.matmul(spread[:], lhsT=group_weights[:], rhs=bias_row[:], start=True, stop=True)
-        nc.vector.tensor_copy(out=group_bias[:], in_=spread[:])
 
-        side = [side_stages(0, first_rows[0], first_rows[1])]
-        side.append(side_stages(1, load_rows(q_blk[1]), load_rows(k_blk[1])))
+        def spread_bias():
+            spread = psum_vsum.tile([P, C], F32, name="spread", tag="vsum")
+            nc.tensor.matmul(spread[:], lhsT=group_weights[:], rhs=bias_row[:], start=True, stop=True)
+            nc.vector.tensor_copy(out=group_bias[:], in_=spread[:])
 
-        for i in range(UNITS_PER_BATCH * (BATCH - 1) + len(side[0])):
-            if i < UNITS:
-                regroup(i)
-                if i % 2 == 1 and i // 2 + RAW_BUFS < BATCH * CHUNKS:
-                    load_chunk(i // 2 + RAW_BUFS)
-            for b in range(BATCH):
-                stage = i - b * UNITS_PER_BATCH
-                if 0 <= stage < len(side[b]):
-                    side[b][stage]()
-            if 1 <= i <= UNITS:
+        one_each = (nc.scalar.copy, nc.vector.tensor_copy)
+        side = [side_stages(0, first_rows[0], first_rows[1], one_each)]
+        side.append(side_stages(1, load_rows(q_blk[1]), load_rows(k_blk[1]), (nc.scalar.copy, nc.scalar.copy)))
+        (
+            flip_q, flip_k, quantise_k, score, maxima_0, maxima_1, exp_0, exp_1, flip_e0, flip_e1, finish_e, group_values, output,
+        ) = range(13)
+        first, last = side
+
+        spread_bias()
+        first[flip_q]()
+        first[flip_k]()
+        first[quantise_k]()
+        flip_rows(wv_rows, wv_grouped, one_each)
+        first[score]()
+        first[maxima_0]()
+        quantise(nc, wv, all_columns, wv_grouped[:].rearrange("p r t -> p (r t)"))
+        regroup(0)
+        first[maxima_1]()
+        first[exp_0]()
+        regroup(1)
+        load_chunk(RAW_BUFS)
+        first[exp_1]()
+        project(0)
+        stage_turns = {
+            2: [(0, flip_e0)], 3: [(0, flip_e1)], 5: [(0, finish_e)],
+            9: [(1, flip_q)], 10: [(0, group_values), (1, flip_k)], 11: [(0, output)],
+            12: [(1, quantise_k), (1, score)], 13: [(1, maxima_0)], 14: [(1, maxima_1)],
+        }
+        for i in range(2, UNITS):
+            if i == UNITS - 1:
                 project(i - 1)
-            if i % 2 == 1 and 0 <= (i - 3) // 2 < BATCH * CHUNKS:
+            regroup(i)
+            if i % 2 == 1 and i // 2 + RAW_BUFS < BATCH * CHUNKS:
+                load_chunk(i // 2 + RAW_BUFS)
+            for b, stage in stage_turns.get(i, ()):
+                side[b][stage]()
+            if i < UNITS - 1:
+                project(i - 1)
+            if i % 2 == 1:
                 leave((i - 3) // 2)
+        last[exp_0]()
+        last[exp_1]()
+        project(UNITS - 1)
+        last[flip_e0]()
+        last[flip_e1]()
+        leave(BATCH * CHUNKS - 1)
+        last[group_values]()
+        last[finish_e]()
+        last[output]()

@@ -26,7 +26,8 @@ RUN = 4
 HALF = GROUP // 2
 UNITS_PER_BATCH = 2 * CHUNKS
 UNITS = BATCH * UNITS_PER_BATCH
-VECTOR_GROUPS = 112
+VECTOR_GROUPS = 120
+VECTOR_CHANNELS = 512
 LAST_SCALAR_GROUPS = 96
 RAW_BUFS = 4
 SCALE = 1.0 / math.sqrt(C)
@@ -66,7 +67,7 @@ def tile_coarseblockattention_pb_kernel(tc, x, q_blk, k_blk, Wv, bv, out):
         raw_pool = ctx.enter_context(tc.tile_pool(name="raw", bufs=RAW_BUFS))
         pixel_pool = ctx.enter_context(tc.tile_pool(name="pixels", bufs=2))
         batch_pool = ctx.enter_context(tc.tile_pool(name="batch", bufs=BATCH))
-        store_pool = ctx.enter_context(tc.tile_pool(name="store", bufs=4))
+        store_pool = ctx.enter_context(tc.tile_pool(name="store", bufs=2 * TILES))
         psum_flip = ctx.enter_context(tc.psum_pool(name="psum_flip", bufs=2))
         psum_vsum = ctx.enter_context(tc.psum_pool(name="psum_vsum", bufs=2))
         psum_wide = ctx.enter_context(tc.psum_pool(name="psum_wide", bufs=TILES))
@@ -210,13 +211,13 @@ def tile_coarseblockattention_pb_kernel(tc, x, q_blk, k_blk, Wv, bv, out):
                 grouped_words = e_grouped[:].bitcast(F32).rearrange("p (h a r) u -> p h a r u", h=2, a=2)
                 flip_half(words[:, 2 * h : 2 * h + 2], grouped_words[:, h], nc.scalar.copy)
 
-            def mix():
+            def mix(exits):
                 for a in range(TILES):
                     queries = slice(a * P, (a + 1) * P)
                     mixed = psum_wide.tile([P, C], F32, name="mixed", tag="wide")
                     matmul_mx(nc, mixed[:], e, queries, values)
                     result = store_pool.tile([P, C], F32, name="result")
-                    if a % 2 == 0:
+                    if exits[a] == "S":
                         nc.scalar.activation(out=result[:], in_=mixed[:], func=ACT.Copy, scale=inv_sum[:, a : a + 1])
                     else:
                         nc.vector.tensor_scalar(
@@ -239,18 +240,25 @@ def tile_coarseblockattention_pb_kernel(tc, x, q_blk, k_blk, Wv, bv, out):
                 nc.vector.reciprocal(out=inv_sum[:], in_=row_sum[:])
 
             def group_values():
-                nc.vector.tensor_copy(out=vsum_grouped[:], in_=vsum_bf16[b][:].rearrange("p t c -> p c t"))
+                spread = vsum_bf16[b][:].rearrange("p t c -> p c t")
+                if b == 0:
+                    nc.scalar.copy(out=vsum_grouped[:], in_=spread)
+                else:
+                    cut = VECTOR_CHANNELS
+                    nc.vector.tensor_copy(out=vsum_grouped[:, :cut], in_=spread[:, :cut])
+
+            def quantise_values():
+                quantise(nc, values, all_columns, vsum_grouped[:].rearrange("p c t -> p (c t)"))
 
             def output():
-                quantise(nc, values, all_columns, vsum_grouped[:].rearrange("p c t -> p (c t)"))
-                mix()
+                mix("SSSS" if b == 0 else "SVSV")
 
             return [
                 flip_q, flip_k, quantise_k, score,
                 lambda: maxima(0), lambda: maxima(1),
                 lambda: exponentials(0), lambda: exponentials(1),
                 lambda: flip_e(0), lambda: flip_e(1),
-                finish_e, group_values, output,
+                finish_e, group_values, quantise_values, output,
             ]
 
         bias_row = const.tile([P, C], BF16, name="bias_row")
@@ -281,14 +289,14 @@ def tile_coarseblockattention_pb_kernel(tc, x, q_blk, k_blk, Wv, bv, out):
         def spread_bias():
             spread = psum_vsum.tile([P, C], F32, name="spread", tag="vsum")
             nc.tensor.matmul(spread[:], lhsT=group_weights[:], rhs=bias_row[:], start=True, stop=True)
-            nc.vector.tensor_copy(out=group_bias[:], in_=spread[:])
+            nc.scalar.copy(out=group_bias[:], in_=spread[:])
 
         one_each = (nc.scalar.copy, nc.vector.tensor_copy)
         side = [side_stages(0, first_rows[0], first_rows[1], one_each)]
         side.append(side_stages(1, load_rows(q_blk[1]), load_rows(k_blk[1]), (nc.scalar.copy, nc.scalar.copy)))
         (
-            flip_q, flip_k, quantise_k, score, maxima_0, maxima_1, exp_0, exp_1, flip_e0, flip_e1, finish_e, group_values, output,
-        ) = range(13)
+            flip_q, flip_k, quantise_k, score, maxima_0, maxima_1, exp_0, exp_1, flip_e0, flip_e1, finish_e, group_values, quantise_values, output,
+        ) = range(14)
         first, last = side
 
         spread_bias()
@@ -307,8 +315,8 @@ def tile_coarseblockattention_pb_kernel(tc, x, q_blk, k_blk, Wv, bv, out):
         first[exp_1]()
         project(0)
         stage_turns = {
-            2: [(0, flip_e0)], 3: [(0, flip_e1)], 5: [(0, finish_e)],
-            9: [(1, flip_q)], 10: [(0, group_values), (1, flip_k)], 11: [(0, output)],
+            2: [(0, flip_e0)], 3: [(0, flip_e1)],
+            9: [(1, flip_q)], 10: [(1, flip_k)],
             12: [(1, quantise_k), (1, score)], 13: [(1, maxima_0)], 14: [(1, maxima_1)],
         }
         for i in range(2, UNITS):
@@ -325,10 +333,15 @@ def tile_coarseblockattention_pb_kernel(tc, x, q_blk, k_blk, Wv, bv, out):
                 leave((i - 3) // 2)
         last[exp_0]()
         last[exp_1]()
+        first[group_values]()
         project(UNITS - 1)
+        first[finish_e]()
+        first[quantise_values]()
         last[flip_e0]()
         last[flip_e1]()
         leave(BATCH * CHUNKS - 1)
         last[group_values]()
+        first[output]()
         last[finish_e]()
+        last[quantise_values]()
         last[output]()

@@ -26,9 +26,8 @@ RUN = 4
 HALF = GROUP // 2
 UNITS_PER_BATCH = 2 * CHUNKS
 UNITS = BATCH * UNITS_PER_BATCH
-VECTOR_GROUPS = 120
 VECTOR_CHANNELS = 512
-LAST_SCALAR_GROUPS = 96
+RUNS = GROUP // RUN
 RAW_BUFS = 4
 SCALE = 1.0 / math.sqrt(C)
 
@@ -76,9 +75,12 @@ def tile_coarseblockattention_pb_kernel(tc, x, q_blk, k_blk, Wv, bv, out):
         all_columns = slice(0, BLOCKS)
         x_quads = x.rearrange("b (p t) h w -> b p t (h w)", t=PACK)
 
-        def load_rows(rows):
+        def load_rows(rows, pieces=1):
             by_row = rows_pool.tile([P, TILES, C], BF16, name="by_row")
-            nc.sync.dma_start(out=by_row[:], in_=rows.rearrange("(a p) c -> p a c", p=P))
+            by_tile = rows.rearrange("(a p) c -> p a c", p=P)
+            step = TILES // pieces
+            for a in range(0, TILES, step):
+                nc.sync.dma_start(out=by_row[:, a : a + step], in_=by_tile[:, a : a + step])
             return by_row
 
         raw = {}
@@ -117,47 +119,28 @@ def tile_coarseblockattention_pb_kernel(tc, x, q_blk, k_blk, Wv, bv, out):
         vsum = {}
         vsum_bf16 = {}
 
-        def regroup(unit):
-            c, h = divmod(unit, 2)
-            if h == 0:
+        def regroup(copy, c, runs, groups=slice(0, P)):
+            if c not in grouped:
                 grouped[c] = pixel_pool.tile([P, GROUP, P, PACK], BF16, name="grouped", align_bytes=64)
-            read = raw[c][:].rearrange("p t (g s i) -> p s g t i", s=GROUP // RUN, i=RUN)
+            read = raw[c][:].rearrange("p t (g s i) -> p s g t i", s=RUNS, i=RUN)
             write = grouped[c][:].rearrange("p (s i) g t -> p s g t i", i=RUN)
+            copy(out=write[:, runs, groups], in_=read[:, runs, groups])
 
-            def copy(engine_copy, s, groups):
-                engine_copy(out=write[:, s, groups], in_=read[:, s, groups])
-
-            if c < 1:
-                groups = slice(h * P // 2, (h + 1) * P // 2)
-                for s in (0, 1):
-                    copy(nc.vector.tensor_copy, s, groups)
-                    copy(nc.scalar.copy, s + 2, groups)
-                return
-            if unit == UNITS - 1:
-                copy(nc.vector.tensor_copy, 2 * h, slice(0, P))
-                copy(nc.scalar.copy, 2 * h + 1, slice(0, LAST_SCALAR_GROUPS))
-                copy(nc.vector.tensor_copy, 2 * h + 1, slice(LAST_SCALAR_GROUPS, P))
-                return
-            copy(nc.vector.tensor_copy, 2 * h, slice(0, VECTOR_GROUPS))
-            copy(nc.scalar.copy, 2 * h + 1, slice(0, P))
-            copy(nc.scalar.copy, 2 * h, slice(VECTOR_GROUPS, P))
-
-        def project(unit):
-            c, h = divmod(unit, 2)
-            if h == 0:
+        def project(c, runs):
+            if c not in pixels:
                 pixels[c] = mx_tiles(pixel_pool, "pixels", GROUP * P)
                 vsum[c] = psum_vsum.tile([P, C], F32, name="vsum")
-            for s in (2 * h, 2 * h + 1):
-                quantise(
-                    nc,
-                    pixels[c],
-                    slice(s * RUN * P, (s + 1) * RUN * P),
-                    grouped[c][:, s * RUN : (s + 1) * RUN, :, :].rearrange("p j g t -> p (j g t)"),
+            planes = slice(runs.start * RUN, runs.stop * RUN)
+            quantise(
+                nc,
+                pixels[c],
+                slice(planes.start * P, planes.stop * P),
+                grouped[c][:, planes].rearrange("p j g t -> p (j g t)"),
+            )
+            for j in range(planes.start, planes.stop):
+                matmul_mx(
+                    nc, vsum[c][:], pixels[c], slice(j * P, (j + 1) * P), wv, start=(j == 0), stop=(j == GROUP - 1)
                 )
-                for j in range(s * RUN, (s + 1) * RUN):
-                    matmul_mx(
-                        nc, vsum[c][:], pixels[c], slice(j * P, (j + 1) * P), wv, start=(j == 0), stop=(j == GROUP - 1)
-                    )
 
         def leave(c):
             b, t = divmod(c, CHUNKS)
@@ -266,13 +249,17 @@ def tile_coarseblockattention_pb_kernel(tc, x, q_blk, k_blk, Wv, bv, out):
         nc.sync.dma_start(out=bias_row[0:1, :], in_=bv.unsqueeze(0))
         group_weights = const.tile([P, P], BF16, name="group_weights")
         nc.vector.memset(group_weights[:], float(GROUP))
-        first_rows = (load_rows(q_blk[0]), load_rows(k_blk[0]))
+        q_first = load_rows(q_blk[0])
+        k_first = load_rows(k_blk[0])
         wv_rows = load_rows(Wv)
-        for c in range(2):
-            for piece in range(2):
-                load_chunk(c, piece, 2)
-        for c in range(2, RAW_BUFS):
-            load_chunk(c)
+        load_chunk(0, 0, 2)
+        load_chunk(0, 1, 2)
+        load_chunk(1, 0, 2)
+        load_chunk(1, 1, 2)
+        load_chunk(2)
+        load_chunk(3)
+        q_last = load_rows(q_blk[1])
+        k_last = load_rows(k_blk[1])
 
         warm = const.tile([P, 1], F32, name="warm")
         nc.vector.memset(warm[:], 0.0)
@@ -292,12 +279,16 @@ def tile_coarseblockattention_pb_kernel(tc, x, q_blk, k_blk, Wv, bv, out):
             nc.scalar.copy(out=group_bias[:], in_=spread[:])
 
         one_each = (nc.scalar.copy, nc.vector.tensor_copy)
-        side = [side_stages(0, first_rows[0], first_rows[1], one_each)]
-        side.append(side_stages(1, load_rows(q_blk[1]), load_rows(k_blk[1]), (nc.scalar.copy, nc.scalar.copy)))
+        side = [side_stages(0, q_first, k_first, one_each)]
+        side.append(side_stages(1, q_last, k_last, (nc.scalar.copy, nc.scalar.copy)))
         (
             flip_q, flip_k, quantise_k, score, maxima_0, maxima_1, exp_0, exp_1, flip_e0, flip_e1, finish_e, group_values, quantise_values, output,
         ) = range(14)
         first, last = side
+
+        by_vector, by_scalar = nc.vector.tensor_copy, nc.scalar.copy
+        front, back = slice(0, 2), slice(2, 4)
+        halves = (slice(0, P // 2), slice(P // 2, P))
 
         spread_bias()
         first[flip_q]()
@@ -307,39 +298,56 @@ def tile_coarseblockattention_pb_kernel(tc, x, q_blk, k_blk, Wv, bv, out):
         first[score]()
         first[maxima_0]()
         quantise(nc, wv, all_columns, wv_grouped[:].rearrange("p r t -> p (r t)"))
-        regroup(0)
+        regroup(by_vector, 0, front, halves[0])
+        regroup(by_scalar, 0, back, halves[0])
         first[maxima_1]()
         first[exp_0]()
-        regroup(1)
+        regroup(by_vector, 0, front, halves[1])
+        regroup(by_scalar, 0, back, halves[1])
         load_chunk(RAW_BUFS)
         first[exp_1]()
-        project(0)
-        stage_turns = {
-            2: [(0, flip_e0)], 3: [(0, flip_e1)],
-            9: [(1, flip_q)], 10: [(1, flip_k)],
-            12: [(1, quantise_k), (1, score)], 13: [(1, maxima_0)], 14: [(1, maxima_1)],
+        project(0, front)
+        stages = {
+            1: [(0, flip_e0), (0, flip_e1)],
+            4: [(1, flip_q)], 5: [(1, flip_k)], 6: [(1, quantise_k), (1, score), (1, maxima_0), (1, maxima_1)],
         }
-        for i in range(2, UNITS):
-            if i == UNITS - 1:
-                project(i - 1)
-            regroup(i)
-            if i % 2 == 1 and i // 2 + RAW_BUFS < BATCH * CHUNKS:
-                load_chunk(i // 2 + RAW_BUFS)
-            for b, stage in stage_turns.get(i, ()):
-                side[b][stage]()
-            if i < UNITS - 1:
-                project(i - 1)
-            if i % 2 == 1:
-                leave((i - 3) // 2)
+        for c in range(1, BATCH * CHUNKS - 1):
+            regroup(by_vector, c, front)
+            if c > 1:
+                leave(c - 2)
+            regroup(by_scalar, c, slice(2, 3))
+            regroup(by_scalar, c, slice(3, 4))
+            for b, stage in stages.get(c, ()):
+                if stage < quantise_k or stage > maxima_1: side[b][stage]()
+            if c + RAW_BUFS < BATCH * CHUNKS:
+                load_chunk(c + RAW_BUFS)
+            if c == 6:
+                last[quantise_k]()
+                last[score]()
+            project(c - 1, back)
+            project(c, front)
+        c = BATCH * CHUNKS - 1
+        regroup(by_vector, c, slice(0, 1))
+        project(c - 1, back)
+        leave(c - 2)
+        project(c, slice(0, 1))
+        regroup(by_scalar, c, slice(1, 2))
+        regroup(by_scalar, c, slice(2, 3))
+        regroup(by_scalar, c, slice(3, 4))
+        first[group_values]()
+        last[maxima_0]()
+        project(c, slice(1, 2))
+        last[maxima_1]()
         last[exp_0]()
         last[exp_1]()
-        first[group_values]()
-        project(UNITS - 1)
-        first[finish_e]()
-        first[quantise_values]()
+        project(c, slice(2, 3))
+        leave(c - 1)
+        project(c, slice(3, 4))
         last[flip_e0]()
         last[flip_e1]()
-        leave(BATCH * CHUNKS - 1)
+        first[finish_e]()
+        first[quantise_values]()
+        leave(c)
         last[group_values]()
         first[output]()
         last[finish_e]()

@@ -75,12 +75,9 @@ def tile_coarseblockattention_pb_kernel(tc, x, q_blk, k_blk, Wv, bv, out):
         all_columns = slice(0, BLOCKS)
         x_quads = x.rearrange("b (p t) h w -> b p t (h w)", t=PACK)
 
-        def load_rows(rows, pieces=1):
+        def load_rows(rows, order):
             by_row = rows_pool.tile([P, TILES, C], BF16, name="by_row")
-            by_tile = rows.rearrange("(a p) c -> p a c", p=P)
-            step = TILES // pieces
-            for a in range(0, TILES, step):
-                nc.sync.dma_start(out=by_row[:, a : a + step], in_=by_tile[:, a : a + step])
+            nc.sync.dma_start(out=by_row[:], in_=rows.rearrange(order + " c -> p a c", a=TILES))
             return by_row
 
         raw = {}
@@ -95,24 +92,27 @@ def tile_coarseblockattention_pb_kernel(tc, x, q_blk, k_blk, Wv, bv, out):
                 out=raw[c][:, :, a : a + width], in_=x_quads[b, :, :, t * CHUNK + a : t * CHUNK + a + width]
             )
 
-        def flip_half(words, grouped, copy, pattern="p a u r -> p a r u"):
+        def flip_half(words, grouped, copy, pattern):
             flipped = psum_flip.tile([P, 2, 2, P], F32, name="flipped")
             for a in range(2):
                 for u in range(2):
                     nc.tensor.transpose(flipped[:, a, u, :], words[:, a, u, :], ident_f32[:])
             copy(out=grouped, in_=flipped[:].rearrange(pattern))
 
-        def flip_rows(by_row, grouped, copies):
+        def flip_rows(by_row, grouped, copies, columns, pattern):
             words = by_row[:].bitcast(F32).rearrange("p a (q u) -> p a u q", u=2)
-            grouped_words = grouped[:].bitcast(F32).rearrange("p (h a r) u -> p h a r u", h=2, a=2)
+            grouped_words = grouped[:].bitcast(F32).rearrange(columns, h=2, a=2)
             for h in range(2):
-                flip_half(words[:, 2 * h : 2 * h + 2], grouped_words[:, h], copies[h])
+                flip_half(words[:, 2 * h : 2 * h + 2], grouped_words[:, h], copies[h], pattern)
+
+        def flip_queries(by_row, grouped, copies):
+            flip_rows(by_row, grouped, copies, "p (h a r) u -> p h a r u", "p a u r -> p a r u")
 
         def flip_keys(by_row, grouped, copies):
-            words = by_row[:].bitcast(F32).rearrange("p a (q u) -> p a u q", u=2)
-            grouped_words = grouped[:].bitcast(F32).rearrange("p (h r a) u -> p h r a u", h=2, a=2)
-            for h in range(2):
-                flip_half(words[:, 2 * h : 2 * h + 2], grouped_words[:, h], copies[h], "p a u r -> p r a u")
+            flip_rows(by_row, grouped, copies, "p (h r a) u -> p h r a u", "p a u r -> p r a u")
+
+        def flip_weights(by_row, grouped, copies):
+            flip_rows(by_row, grouped, copies, "p (r h a) u -> p h r a u", "p a u r -> p r a u")
 
         grouped = {}
         pixels = {}
@@ -192,7 +192,7 @@ def tile_coarseblockattention_pb_kernel(tc, x, q_blk, k_blk, Wv, bv, out):
             def flip_e(h):
                 words = e_bf16[:].bitcast(F32).rearrange("p a (u q) -> p a u q", u=2)
                 grouped_words = e_grouped[:].bitcast(F32).rearrange("p (h a r) u -> p h a r u", h=2, a=2)
-                flip_half(words[:, 2 * h : 2 * h + 2], grouped_words[:, h], nc.scalar.copy)
+                flip_half(words[:, 2 * h : 2 * h + 2], grouped_words[:, h], nc.scalar.copy, "p a u r -> p a r u")
 
             def mix(exits):
                 for a in range(TILES):
@@ -206,10 +206,10 @@ def tile_coarseblockattention_pb_kernel(tc, x, q_blk, k_blk, Wv, bv, out):
                         nc.vector.tensor_scalar(
                             out=result[:], in0=mixed[:], scalar1=inv_sum[:, a : a + 1], scalar2=None, op0=ALU.mult
                         )
-                    nc.sync.dma_start(out=out[b, queries, :], in_=result[:])
+                    nc.sync.dma_start(out=out[b].rearrange("(p a) c -> p a c", a=TILES)[:, a], in_=result[:])
 
             def flip_q():
-                flip_rows(q_rows, q_grouped, copies)
+                flip_queries(q_rows, q_grouped, copies)
 
             def flip_k():
                 quantise(nc, q, all_columns, q_grouped[:].rearrange("p r t -> p (r t)"))
@@ -249,17 +249,17 @@ def tile_coarseblockattention_pb_kernel(tc, x, q_blk, k_blk, Wv, bv, out):
         nc.sync.dma_start(out=bias_row[0:1, :], in_=bv.unsqueeze(0))
         group_weights = const.tile([P, P], BF16, name="group_weights")
         nc.vector.memset(group_weights[:], float(GROUP))
-        q_first = load_rows(q_blk[0])
-        k_first = load_rows(k_blk[0])
-        wv_rows = load_rows(Wv)
+        q_first = load_rows(q_blk[0], "(p a)")
+        k_first = load_rows(k_blk[0], "(a p)")
+        wv_rows = load_rows(Wv, "(p a)")
         load_chunk(0, 0, 2)
         load_chunk(0, 1, 2)
         load_chunk(1, 0, 2)
         load_chunk(1, 1, 2)
         load_chunk(2)
         load_chunk(3)
-        q_last = load_rows(q_blk[1])
-        k_last = load_rows(k_blk[1])
+        q_last = load_rows(q_blk[1], "(p a)")
+        k_last = load_rows(k_blk[1], "(a p)")
 
         warm = const.tile([P, 1], F32, name="warm")
         nc.vector.memset(warm[:], 0.0)
@@ -294,7 +294,7 @@ def tile_coarseblockattention_pb_kernel(tc, x, q_blk, k_blk, Wv, bv, out):
         first[flip_q]()
         first[flip_k]()
         first[quantise_k]()
-        flip_rows(wv_rows, wv_grouped, one_each)
+        flip_weights(wv_rows, wv_grouped, one_each)
         first[score]()
         first[maxima_0]()
         quantise(nc, wv, all_columns, wv_grouped[:].rearrange("p r t -> p (r t)"))
@@ -315,8 +315,7 @@ def tile_coarseblockattention_pb_kernel(tc, x, q_blk, k_blk, Wv, bv, out):
             regroup(by_vector, c, front)
             if c > 1:
                 leave(c - 2)
-            regroup(by_scalar, c, slice(2, 3))
-            regroup(by_scalar, c, slice(3, 4))
+            regroup(by_scalar, c, back)
             for b, stage in stages.get(c, ()):
                 if stage < quantise_k or stage > maxima_1: side[b][stage]()
             if c + RAW_BUFS < BATCH * CHUNKS:

@@ -312,7 +312,12 @@ def tile_coarseblockattention_pb_kernel(tc, x, q_blk, k_blk, Wv, bv, out):
             4: [(1, flip_q)], 5: [(1, flip_k)], 6: [(1, quantise_k), (1, score), (1, maxima_0), (1, maxima_1)],
         }
         for c in range(1, BATCH * CHUNKS - 1):
-            regroup(by_vector, c, front)
+            if c in (3,):
+                regroup(by_vector, c, slice(0, 1))
+                regroup(by_vector, c, slice(1, 2), slice(0, 64))
+                regroup(by_scalar, c, slice(1, 2), slice(64, P))
+            else:
+                regroup(by_vector, c, front)
             if c > 1:
                 leave(c - 2)
             regroup(by_scalar, c, back)

@@ -119,12 +119,20 @@ def tile_coarseblockattention_pb_kernel(tc, x, q_blk, k_blk, Wv, bv, out):
         vsum = {}
         vsum_bf16 = {}
 
+        by_vector, by_scalar = nc.vector.tensor_copy, nc.scalar.copy
+
         def regroup(copy, c, runs, groups=slice(0, P)):
             if c not in grouped:
                 grouped[c] = pixel_pool.tile([P, GROUP, P, PACK], BF16, name="grouped", align_bytes=64)
-            read = raw[c][:].rearrange("p t (g s i) -> p s g t i", s=RUNS, i=RUN)
-            write = grouped[c][:].rearrange("p (s i) g t -> p s g t i", i=RUN)
-            copy(out=write[:, runs, groups], in_=read[:, runs, groups])
+            if copy is by_vector:
+                read = raw[c][:].rearrange("p t (g s i) -> p s g t i", s=RUNS, i=RUN)
+                write = grouped[c][:].rearrange("p (s i) g t -> p s g t i", i=RUN)
+                copy(out=write[:, runs, groups], in_=read[:, runs, groups])
+                return
+            read = raw[c][:].rearrange("p (q e) (g s i) -> p s g q i e", e=2, s=RUNS, i=RUN)
+            write = grouped[c][:].rearrange("p (s i) g (q e) -> p s g q i e", e=2, i=RUN)
+            for s in range(runs.start, runs.stop):
+                copy(out=write[:, s, groups], in_=read[:, s, groups])
 
         def project(c, runs):
             if c not in pixels:
@@ -286,7 +294,6 @@ def tile_coarseblockattention_pb_kernel(tc, x, q_blk, k_blk, Wv, bv, out):
         ) = range(14)
         first, last = side
 
-        by_vector, by_scalar = nc.vector.tensor_copy, nc.scalar.copy
         front, back = slice(0, 2), slice(2, 4)
         halves = (slice(0, P // 2), slice(P // 2, P))
 

@@ -124,11 +124,6 @@ def tile_coarseblockattention_pb_kernel(tc, x, q_blk, k_blk, Wv, bv, out):
         def regroup(copy, c, runs, groups=slice(0, P)):
             if c not in grouped:
                 grouped[c] = pixel_pool.tile([P, GROUP, P, PACK], BF16, name="grouped", align_bytes=64)
-            if copy is by_vector:
-                read = raw[c][:].rearrange("p t (g s i) -> p s g t i", s=RUNS, i=RUN)
-                write = grouped[c][:].rearrange("p (s i) g t -> p s g t i", i=RUN)
-                copy(out=write[:, runs, groups], in_=read[:, runs, groups])
-                return
             read = raw[c][:].rearrange("p (q e) (g s i) -> p s g q i e", e=2, s=RUNS, i=RUN)
             write = grouped[c][:].rearrange("p (s i) g (q e) -> p s g q i e", e=2, i=RUN)
             for s in range(runs.start, runs.stop):

@@ -22,14 +22,16 @@ BLOCKS = PIXELS // GROUP
 TILES = BLOCKS // P
 CHUNK = P * GROUP
 CHUNKS = PIXELS // CHUNK
+ALL_CHUNKS = BATCH * CHUNKS
+LAST = ALL_CHUNKS - 1
 RUN = 4
-HALF = GROUP // 2
-UNITS_PER_BATCH = 2 * CHUNKS
-UNITS = BATCH * UNITS_PER_BATCH
-VECTOR_CHANNELS = 512
 RUNS = GROUP // RUN
 RAW_BUFS = 4
 SCALE = 1.0 / math.sqrt(C)
+
+VECTOR_RUNS = 2
+EVEN_OUT = 3
+EVEN_GROUPS = 96
 
 FLOPS = 2 * BATCH * (PIXELS * C * C + 2 * BLOCKS * BLOCKS * C)
 
@@ -66,12 +68,13 @@ def tile_coarseblockattention_pb_kernel(tc, x, q_blk, k_blk, Wv, bv, out):
         raw_pool = ctx.enter_context(tc.tile_pool(name="raw", bufs=RAW_BUFS))
         pixel_pool = ctx.enter_context(tc.tile_pool(name="pixels", bufs=2))
         batch_pool = ctx.enter_context(tc.tile_pool(name="batch", bufs=BATCH))
-        store_pool = ctx.enter_context(tc.tile_pool(name="store", bufs=2 * TILES))
+        store_pool = ctx.enter_context(tc.tile_pool(name="store", bufs=BATCH * TILES))
         psum_flip = ctx.enter_context(tc.psum_pool(name="psum_flip", bufs=2))
         psum_vsum = ctx.enter_context(tc.psum_pool(name="psum_vsum", bufs=2))
         psum_wide = ctx.enter_context(tc.psum_pool(name="psum_wide", bufs=TILES))
-
         ctx.enter_context(tc.manual_schedule())
+
+        by_vector, by_scalar = nc.vector.tensor_copy, nc.scalar.copy
         all_columns = slice(0, BLOCKS)
         x_quads = x.rearrange("b (p t) h w -> b p t (h w)", t=PACK)
 
@@ -87,20 +90,21 @@ def tile_coarseblockattention_pb_kernel(tc, x, q_blk, k_blk, Wv, bv, out):
             if piece == 0:
                 raw[c] = raw_pool.tile([P, PACK, CHUNK], BF16, name="raw")
             width = CHUNK // pieces
-            a = piece * width
+            offset = piece * width
             nc.sync.dma_start(
-                out=raw[c][:, :, a : a + width], in_=x_quads[b, :, :, t * CHUNK + a : t * CHUNK + a + width]
+                out=raw[c][:, :, offset : offset + width],
+                in_=x_quads[b, :, :, t * CHUNK + offset : t * CHUNK + offset + width],
             )
 
         def flip_half(words, grouped, copy, pattern):
             flipped = psum_flip.tile([P, 2, 2, P], F32, name="flipped")
             for a in range(2):
                 for u in range(2):
-                    nc.tensor.transpose(flipped[:, a, u, :], words[:, a, u, :], ident_f32[:])
+                    nc.tensor.transpose(flipped[:, a, u, :], words[:, a, u, :], ident[:])
             copy(out=grouped, in_=flipped[:].rearrange(pattern))
 
         def flip_rows(by_row, grouped, copies, columns, pattern):
-            words = by_row[:].bitcast(F32).rearrange("p a (q u) -> p a u q", u=2)
+            words = by_row[:].bitcast(F32).rearrange("p a (n u) -> p a u n", u=2)
             grouped_words = grouped[:].bitcast(F32).rearrange(columns, h=2, a=2)
             for h in range(2):
                 flip_half(words[:, 2 * h : 2 * h + 2], grouped_words[:, h], copies[h], pattern)
@@ -119,13 +123,11 @@ def tile_coarseblockattention_pb_kernel(tc, x, q_blk, k_blk, Wv, bv, out):
         vsum = {}
         vsum_bf16 = {}
 
-        by_vector, by_scalar = nc.vector.tensor_copy, nc.scalar.copy
-
         def regroup(copy, c, runs, groups=slice(0, P)):
             if c not in grouped:
                 grouped[c] = pixel_pool.tile([P, GROUP, P, PACK], BF16, name="grouped", align_bytes=64)
-            read = raw[c][:].rearrange("p (q e) (g s i) -> p s g q i e", e=2, s=RUNS, i=RUN)
-            write = grouped[c][:].rearrange("p (s i) g (q e) -> p s g q i e", e=2, i=RUN)
+            read = raw[c][:].rearrange("p (n e) (g s i) -> p s g n i e", e=2, s=RUNS, i=RUN)
+            write = grouped[c][:].rearrange("p (s i) g (n e) -> p s g n i e", e=2, i=RUN)
             for s in range(runs.start, runs.stop):
                 copy(out=write[:, s, groups], in_=read[:, s, groups])
 
@@ -133,14 +135,14 @@ def tile_coarseblockattention_pb_kernel(tc, x, q_blk, k_blk, Wv, bv, out):
             if c not in pixels:
                 pixels[c] = mx_tiles(pixel_pool, "pixels", GROUP * P)
                 vsum[c] = psum_vsum.tile([P, C], F32, name="vsum")
-            planes = slice(runs.start * RUN, runs.stop * RUN)
+            low, high = runs.start * RUN, runs.stop * RUN
             quantise(
                 nc,
                 pixels[c],
-                slice(planes.start * P, planes.stop * P),
-                grouped[c][:, planes].rearrange("p j g t -> p (j g t)"),
+                slice(low * P, high * P),
+                grouped[c][:, low:high].rearrange("p j g t -> p (j g t)"),
             )
-            for j in range(planes.start, planes.stop):
+            for j in range(low, high):
                 matmul_mx(
                     nc, vsum[c][:], pixels[c], slice(j * P, (j + 1) * P), wv, start=(j == 0), stop=(j == GROUP - 1)
                 )
@@ -149,7 +151,7 @@ def tile_coarseblockattention_pb_kernel(tc, x, q_blk, k_blk, Wv, bv, out):
             b, t = divmod(c, CHUNKS)
             nc.vector.tensor_tensor(out=vsum_bf16[b][:, t, :], in0=vsum[c][:], in1=group_bias[:], op=ALU.add)
 
-        def side_stages(b, q_rows, k_rows, copies):
+        def attention(b, q_rows, k_rows, copies):
             q = mx_tiles(batch_pool, "q", BLOCKS)
             k = mx_tiles(batch_pool, "k", BLOCKS)
             e = mx_tiles(batch_pool, "e", BLOCKS)
@@ -165,6 +167,18 @@ def tile_coarseblockattention_pb_kernel(tc, x, q_blk, k_blk, Wv, bv, out):
             e_bf16 = batch_pool.tile([P, TILES, BLOCKS], BF16, name="e_bf16")
             vsum_bf16[b] = batch_pool.tile([P, CHUNKS, C], BF16, name="vsum_bf16")
             scores = {}
+
+            def flip_q():
+                flip_queries(q_rows, q_grouped, copies)
+
+            def quantise_q():
+                quantise(nc, q, all_columns, q_grouped[:].rearrange("p r t -> p (r t)"))
+
+            def flip_k():
+                flip_keys(k_rows, k_grouped, copies)
+
+            def quantise_k():
+                quantise(nc, k, all_columns, k_grouped[:].rearrange("p r t -> p (r t)"))
 
             def score():
                 for a in range(TILES):
@@ -193,17 +207,29 @@ def tile_coarseblockattention_pb_kernel(tc, x, q_blk, k_blk, Wv, bv, out):
                     )
 
             def flip_e(h):
-                words = e_bf16[:].bitcast(F32).rearrange("p a (u q) -> p a u q", u=2)
+                words = e_bf16[:].bitcast(F32).rearrange("p a (u n) -> p a u n", u=2)
                 grouped_words = e_grouped[:].bitcast(F32).rearrange("p (h a r) u -> p h a r u", h=2, a=2)
-                flip_half(words[:, 2 * h : 2 * h + 2], grouped_words[:, h], nc.scalar.copy, "p a u r -> p a r u")
+                flip_half(words[:, 2 * h : 2 * h + 2], grouped_words[:, h], by_scalar, "p a u r -> p a r u")
+
+            def quantise_e():
+                quantise(nc, e, all_columns, e_grouped[:].rearrange("p n t -> p (n t)"))
+                nc.vector.reciprocal(out=inv_sum[:], in_=row_sum[:])
+
+            def group_values(copy):
+                copy(
+                    out=vsum_grouped[:].rearrange("p (m i) (n e) -> p m n i e", i=RUN, e=2),
+                    in_=vsum_bf16[b][:].rearrange("p (n e) (m i) -> p m n i e", i=RUN, e=2),
+                )
+
+            def quantise_values():
+                quantise(nc, values, all_columns, vsum_grouped[:].rearrange("p c t -> p (c t)"))
 
             def mix(exits):
                 for a in range(TILES):
-                    queries = slice(a * P, (a + 1) * P)
                     mixed = psum_wide.tile([P, C], F32, name="mixed", tag="wide")
-                    matmul_mx(nc, mixed[:], e, queries, values)
+                    matmul_mx(nc, mixed[:], e, slice(a * P, (a + 1) * P), values)
                     result = store_pool.tile([P, C], F32, name="result")
-                    if exits[a] == "S":
+                    if exits[a] == by_scalar:
                         nc.scalar.activation(out=result[:], in_=mixed[:], func=ACT.Copy, scale=inv_sum[:, a : a + 1])
                     else:
                         nc.vector.tensor_scalar(
@@ -211,151 +237,115 @@ def tile_coarseblockattention_pb_kernel(tc, x, q_blk, k_blk, Wv, bv, out):
                         )
                     nc.sync.dma_start(out=out[b].rearrange("(p a) c -> p a c", a=TILES)[:, a], in_=result[:])
 
-            def flip_q():
-                flip_queries(q_rows, q_grouped, copies)
-
-            def flip_k():
-                quantise(nc, q, all_columns, q_grouped[:].rearrange("p r t -> p (r t)"))
-                flip_keys(k_rows, k_grouped, copies)
-
-            def quantise_k():
-                quantise(nc, k, all_columns, k_grouped[:].rearrange("p r t -> p (r t)"))
-
-            def finish_e():
-                quantise(nc, e, all_columns, e_grouped[:].rearrange("p n t -> p (n t)"))
-                nc.vector.reciprocal(out=inv_sum[:], in_=row_sum[:])
-
-            def group_values():
-                spread = vsum_bf16[b][:].rearrange("p t c -> p c t")
-                if b == 0:
-                    nc.scalar.copy(out=vsum_grouped[:], in_=spread)
-                else:
-                    cut = VECTOR_CHANNELS
-                    nc.vector.tensor_copy(out=vsum_grouped[:, :cut], in_=spread[:, :cut])
-
-            def quantise_values():
-                quantise(nc, values, all_columns, vsum_grouped[:].rearrange("p c t -> p (c t)"))
-
-            def output():
-                mix("SSSS" if b == 0 else "SVSV")
-
-            return [
-                flip_q, flip_k, quantise_k, score,
-                lambda: maxima(0), lambda: maxima(1),
-                lambda: exponentials(0), lambda: exponentials(1),
-                lambda: flip_e(0), lambda: flip_e(1),
-                finish_e, group_values, quantise_values, output,
-            ]
+            return {
+                "flip_q": flip_q, "quantise_q": quantise_q, "flip_k": flip_k, "quantise_k": quantise_k,
+                "score": score, "maxima": maxima, "exponentials": exponentials, "flip_e": flip_e,
+                "quantise_e": quantise_e, "group_values": group_values, "quantise_values": quantise_values, "mix": mix,
+            }
 
         bias_row = const.tile([P, C], BF16, name="bias_row")
         nc.vector.memset(bias_row[:], 0.0)
         nc.sync.dma_start(out=bias_row[0:1, :], in_=bv.unsqueeze(0))
         group_weights = const.tile([P, P], BF16, name="group_weights")
         nc.vector.memset(group_weights[:], float(GROUP))
-        q_first = load_rows(q_blk[0], "(p a)")
-        k_first = load_rows(k_blk[0], "(a p)")
+
+        q_rows, k_rows = load_rows(q_blk[0], "(p a)"), load_rows(k_blk[0], "(a p)")
         wv_rows = load_rows(Wv, "(p a)")
-        load_chunk(0, 0, 2)
-        load_chunk(0, 1, 2)
-        load_chunk(1, 0, 2)
-        load_chunk(1, 1, 2)
-        load_chunk(2)
-        load_chunk(3)
-        q_last = load_rows(q_blk[1], "(p a)")
-        k_last = load_rows(k_blk[1], "(a p)")
+        for c in range(2):
+            for piece in range(2):
+                load_chunk(c, piece, 2)
+        for c in range(2, RAW_BUFS):
+            load_chunk(c)
 
         warm = const.tile([P, 1], F32, name="warm")
         nc.vector.memset(warm[:], 0.0)
         nc.scalar.activation(out=warm[:], in_=warm[:], func=ACT.Exp)
 
-        ident_f32 = const.tile([P, P], F32, name="ident_f32")
-        make_identity(nc, ident_f32[:])
+        ident = const.tile([P, P], F32, name="ident")
+        make_identity(nc, ident[:])
+
+        group_bias = const.tile([P, C], F32, name="group_bias")
+        spread = psum_vsum.tile([P, C], F32, name="spread", tag="vsum")
+        nc.tensor.matmul(spread[:], lhsT=group_weights[:], rhs=bias_row[:], start=True, stop=True)
+        nc.scalar.copy(out=group_bias[:], in_=spread[:])
 
         wv = mx_tiles(const, "wv", C)
         wv_grouped = const.tile([P, C, PACK], BF16, name="wv_grouped", align_bytes=64)
+        vector_runs, scalar_runs = slice(0, VECTOR_RUNS), slice(VECTOR_RUNS, RUNS)
+        one_each = (by_scalar, by_vector)
 
-        group_bias = const.tile([P, C], F32, name="group_bias")
-
-        def spread_bias():
-            spread = psum_vsum.tile([P, C], F32, name="spread", tag="vsum")
-            nc.tensor.matmul(spread[:], lhsT=group_weights[:], rhs=bias_row[:], start=True, stop=True)
-            nc.scalar.copy(out=group_bias[:], in_=spread[:])
-
-        one_each = (nc.scalar.copy, nc.vector.tensor_copy)
-        side = [side_stages(0, q_first, k_first, one_each)]
-        side.append(side_stages(1, q_last, k_last, (nc.scalar.copy, nc.scalar.copy)))
-        (
-            flip_q, flip_k, quantise_k, score, maxima_0, maxima_1, exp_0, exp_1, flip_e0, flip_e1, finish_e, group_values, quantise_values, output,
-        ) = range(14)
-        first, last = side
-
-        front, back = slice(0, 2), slice(2, 4)
-        halves = (slice(0, P // 2), slice(P // 2, P))
-
-        spread_bias()
-        first[flip_q]()
-        first[flip_k]()
-        first[quantise_k]()
+        first = attention(0, q_rows, k_rows, one_each)
+        first["flip_q"]()
+        first["quantise_q"]()
+        first["flip_k"]()
+        first["quantise_k"]()
         flip_weights(wv_rows, wv_grouped, one_each)
-        first[score]()
-        first[maxima_0]()
+        first["score"]()
+        first["maxima"](0)
         quantise(nc, wv, all_columns, wv_grouped[:].rearrange("p r t -> p (r t)"))
-        regroup(by_vector, 0, front, halves[0])
-        regroup(by_scalar, 0, back, halves[0])
-        first[maxima_1]()
-        first[exp_0]()
-        regroup(by_vector, 0, front, halves[1])
-        regroup(by_scalar, 0, back, halves[1])
+        for h in range(2):
+            half = slice(h * P // 2, (h + 1) * P // 2)
+            regroup(by_vector, 0, vector_runs, half)
+            regroup(by_scalar, 0, scalar_runs, half)
+            if h == 0:
+                first["maxima"](1)
+            first["exponentials"](h)
         load_chunk(RAW_BUFS)
-        first[exp_1]()
-        project(0, front)
-        stages = {
-            1: [(0, flip_e0), (0, flip_e1)],
-            4: [(1, flip_q)], 5: [(1, flip_k)], 6: [(1, quantise_k), (1, score), (1, maxima_0), (1, maxima_1)],
-        }
-        for c in range(1, BATCH * CHUNKS - 1):
-            if c in (3,):
+        project(0, vector_runs)
+
+        for c in range(1, LAST):
+            if c == EVEN_OUT:
                 regroup(by_vector, c, slice(0, 1))
-                regroup(by_vector, c, slice(1, 2), slice(0, 64))
-                regroup(by_scalar, c, slice(1, 2), slice(64, P))
+                regroup(by_vector, c, slice(1, 2), slice(0, EVEN_GROUPS))
+                regroup(by_scalar, c, slice(1, 2), slice(EVEN_GROUPS, P))
             else:
-                regroup(by_vector, c, front)
+                regroup(by_vector, c, vector_runs)
             if c > 1:
                 leave(c - 2)
-            regroup(by_scalar, c, back)
-            for b, stage in stages.get(c, ()):
-                if stage < quantise_k or stage > maxima_1: side[b][stage]()
-            if c + RAW_BUFS < BATCH * CHUNKS:
+            regroup(by_scalar, c, scalar_runs)
+
+            if c == 1:
+                first["flip_e"](0)
+                first["flip_e"](1)
+            if c == CHUNKS:
+                last["flip_q"]()
+            if c == CHUNKS + 1:
+                last["quantise_q"]()
+                last["flip_k"]()
+
+            if c + RAW_BUFS < ALL_CHUNKS:
                 load_chunk(c + RAW_BUFS)
-            if c == 6:
-                last[quantise_k]()
-                last[score]()
-            project(c - 1, back)
-            project(c, front)
-        c = BATCH * CHUNKS - 1
-        regroup(by_vector, c, slice(0, 1))
-        project(c - 1, back)
-        leave(c - 2)
-        project(c, slice(0, 1))
-        regroup(by_scalar, c, slice(1, 2))
-        regroup(by_scalar, c, slice(2, 3))
-        regroup(by_scalar, c, slice(3, 4))
-        first[group_values]()
-        last[maxima_0]()
-        project(c, slice(1, 2))
-        last[maxima_1]()
-        last[exp_0]()
-        last[exp_1]()
-        project(c, slice(2, 3))
-        leave(c - 1)
-        project(c, slice(3, 4))
-        last[flip_e0]()
-        last[flip_e1]()
-        first[finish_e]()
-        first[quantise_values]()
-        leave(c)
-        last[group_values]()
-        first[output]()
-        last[finish_e]()
-        last[quantise_values]()
-        last[output]()
+            if c == 1:
+                q_rows, k_rows = load_rows(q_blk[1], "(p a)"), load_rows(k_blk[1], "(a p)")
+                last = attention(1, q_rows, k_rows, (by_scalar, by_scalar))
+
+            if c == LAST - 1:
+                last["quantise_k"]()
+                last["score"]()
+            project(c - 1, scalar_runs)
+            project(c, vector_runs)
+
+        regroup(by_vector, LAST, slice(0, 1))
+        project(LAST - 1, scalar_runs)
+        leave(LAST - 2)
+        project(LAST, slice(0, 1))
+        regroup(by_scalar, LAST, slice(1, RUNS))
+        first["group_values"](by_scalar)
+        last["maxima"](0)
+        project(LAST, slice(1, 2))
+        last["maxima"](1)
+        last["exponentials"](0)
+        last["exponentials"](1)
+        project(LAST, slice(2, 3))
+        leave(LAST - 1)
+        project(LAST, slice(3, 4))
+        last["flip_e"](0)
+        last["flip_e"](1)
+        first["quantise_e"]()
+        first["quantise_values"]()
+        leave(LAST)
+        last["group_values"](by_vector)
+        first["mix"]((by_scalar,) * TILES)
+        last["quantise_e"]()
+        last["quantise_values"]()
+        last["mix"]((by_scalar, by_vector) * (TILES // 2))

import math
from contextlib import ExitStack

import concourse.mybir as mybir
from concourse.masks import make_identity

F32 = mybir.dt.float32
BF16 = mybir.dt.bfloat16
U32 = mybir.dt.uint32
U8 = mybir.dt.uint8
FP8X4 = mybir.dt.float8_e4m3fn_x4
ALU = mybir.AluOpType
ACT = mybir.ActivationFunctionType

P = 128
PACK = 4
BATCH = 2
C = 512
PIXELS = 128 * 64
GROUP = 16
BLOCKS = PIXELS // GROUP
TILES = BLOCKS // P
CHUNK = P * GROUP
CHUNKS = PIXELS // CHUNK
ALL_CHUNKS = BATCH * CHUNKS
LAST = ALL_CHUNKS - 1
RUN = 4
RUNS = GROUP // RUN
RAW_BUFS = 4
SCALE = 1.0 / math.sqrt(C)

VECTOR_RUNS = 2
EVEN_OUT = 3
EVEN_GROUPS = 96

FLOPS = 2 * BATCH * (PIXELS * C * C + 2 * BLOCKS * BLOCKS * C)


def mx_tiles(pool, name, columns):
    codes = pool.tile([P, columns], U32, name=name + "_codes", align_bytes=64)
    scales = pool.tile([P, columns], U8, name=name + "_scales", align_bytes=64)
    return codes, scales


def quantise(nc, operand, columns, grouped):
    nc.vector.quantize_mx(
        out=operand[0][:, columns].bitcast(FP8X4), scales=operand[1][:, columns], in_=grouped
    )


def matmul_mx(nc, acc, stationary, columns, moving, start=True, stop=True):
    nc.tensor.matmul_mx(
        out=acc,
        lhsT=stationary[0][:, columns].bitcast(FP8X4),
        lhsT_scale=stationary[1][:, columns],
        rhs=moving[0][:].bitcast(FP8X4),
        rhs_scale=moving[1][:],
        start=start,
        stop=stop,
    )


def tile_coarseblockattention_pb_kernel(tc, x, q_blk, k_blk, Wv, bv, out):
    nc = tc.nc
    with ExitStack() as ctx:
        const = ctx.enter_context(tc.tile_pool(name="const", bufs=1))
        rows_pool = ctx.enter_context(tc.tile_pool(name="rows", bufs=1 + 2 * BATCH))
        raw_pool = ctx.enter_context(tc.tile_pool(name="raw", bufs=RAW_BUFS))
        pixel_pool = ctx.enter_context(tc.tile_pool(name="pixels", bufs=2))
        batch_pool = ctx.enter_context(tc.tile_pool(name="batch", bufs=BATCH))
        store_pool = ctx.enter_context(tc.tile_pool(name="store", bufs=BATCH * TILES))
        psum_flip = ctx.enter_context(tc.psum_pool(name="psum_flip", bufs=2))
        psum_vsum = ctx.enter_context(tc.psum_pool(name="psum_vsum", bufs=2))
        psum_wide = ctx.enter_context(tc.psum_pool(name="psum_wide", bufs=TILES))
        ctx.enter_context(tc.manual_schedule())

        by_vector, by_scalar = nc.vector.tensor_copy, nc.scalar.copy
        all_columns = slice(0, BLOCKS)
        x_quads = x.rearrange("b (p t) h w -> b p t (h w)", t=PACK)

        def load_rows(rows, order):
            by_row = rows_pool.tile([P, TILES, C], BF16, name="by_row")
            nc.sync.dma_start(out=by_row[:], in_=rows.rearrange(order + " c -> p a c", a=TILES))
            return by_row

        raw = {}

        def load_chunk(c, piece=0, pieces=1):
            b, t = divmod(c, CHUNKS)
            if piece == 0:
                raw[c] = raw_pool.tile([P, PACK, CHUNK], BF16, name="raw")
            width = CHUNK // pieces
            offset = piece * width
            nc.sync.dma_start(
                out=raw[c][:, :, offset : offset + width],
                in_=x_quads[b, :, :, t * CHUNK + offset : t * CHUNK + offset + width],
            )

        def flip_half(words, grouped, copy, pattern):
            flipped = psum_flip.tile([P, 2, 2, P], F32, name="flipped")
            for a in range(2):
                for u in range(2):
                    nc.tensor.transpose(flipped[:, a, u, :], words[:, a, u, :], ident[:])
            copy(out=grouped, in_=flipped[:].rearrange(pattern))

        def flip_rows(by_row, grouped, copies, columns, pattern):
            words = by_row[:].bitcast(F32).rearrange("p a (n u) -> p a u n", u=2)
            grouped_words = grouped[:].bitcast(F32).rearrange(columns, h=2, a=2)
            for h in range(2):
                flip_half(words[:, 2 * h : 2 * h + 2], grouped_words[:, h], copies[h], pattern)

        def flip_queries(by_row, grouped, copies):
            flip_rows(by_row, grouped, copies, "p (h a r) u -> p h a r u", "p a u r -> p a r u")

        def flip_keys(by_row, grouped, copies):
            flip_rows(by_row, grouped, copies, "p (h r a) u -> p h r a u", "p a u r -> p r a u")

        def flip_weights(by_row, grouped, copies):
            flip_rows(by_row, grouped, copies, "p (r h a) u -> p h r a u", "p a u r -> p r a u")

        grouped = {}
        pixels = {}
        vsum = {}
        vsum_bf16 = {}

        def regroup(copy, c, runs, groups=slice(0, P)):
            if c not in grouped:
                grouped[c] = pixel_pool.tile([P, GROUP, P, PACK], BF16, name="grouped", align_bytes=64)
            read = raw[c][:].rearrange("p (n e) (g s i) -> p s g n i e", e=2, s=RUNS, i=RUN)
            write = grouped[c][:].rearrange("p (s i) g (n e) -> p s g n i e", e=2, i=RUN)
            for s in range(runs.start, runs.stop):
                copy(out=write[:, s, groups], in_=read[:, s, groups])

        def project(c, runs):
            if c not in pixels:
                pixels[c] = mx_tiles(pixel_pool, "pixels", GROUP * P)
                vsum[c] = psum_vsum.tile([P, C], F32, name="vsum")
            low, high = runs.start * RUN, runs.stop * RUN
            quantise(
                nc,
                pixels[c],
                slice(low * P, high * P),
                grouped[c][:, low:high].rearrange("p j g t -> p (j g t)"),
            )
            for j in range(low, high):
                matmul_mx(
                    nc, vsum[c][:], pixels[c], slice(j * P, (j + 1) * P), wv, start=(j == 0), stop=(j == GROUP - 1)
                )

        def leave(c):
            b, t = divmod(c, CHUNKS)
            nc.vector.tensor_tensor(out=vsum_bf16[b][:, t, :], in0=vsum[c][:], in1=group_bias[:], op=ALU.add)

        def attention(b, q_rows, k_rows, copies):
            q = mx_tiles(batch_pool, "q", BLOCKS)
            k = mx_tiles(batch_pool, "k", BLOCKS)
            e = mx_tiles(batch_pool, "e", BLOCKS)
            values = mx_tiles(batch_pool, "values", C)
            q_grouped = batch_pool.tile([P, BLOCKS, PACK], BF16, name="q_grouped", align_bytes=64)
            k_grouped = batch_pool.tile([P, BLOCKS, PACK], BF16, name="k_grouped", align_bytes=64)
            e_grouped = batch_pool.tile([P, BLOCKS, PACK], BF16, name="e_grouped", align_bytes=64)
            vsum_grouped = batch_pool.tile([P, C, PACK], BF16, name="vsum_grouped", align_bytes=64)
            row_max = batch_pool.tile([P, TILES], F32, name="row_max")
            exp_bias = batch_pool.tile([P, TILES], F32, name="exp_bias")
            row_sum = batch_pool.tile([P, TILES], F32, name="row_sum")
            inv_sum = batch_pool.tile([P, TILES], F32, name="inv_sum")
            e_bf16 = batch_pool.tile([P, TILES, BLOCKS], BF16, name="e_bf16")
            vsum_bf16[b] = batch_pool.tile([P, CHUNKS, C], BF16, name="vsum_bf16")
            scores = {}

            def flip_q():
                flip_queries(q_rows, q_grouped, copies)

            def quantise_q():
                quantise(nc, q, all_columns, q_grouped[:].rearrange("p r t -> p (r t)"))

            def flip_k():
                flip_keys(k_rows, k_grouped, copies)

            def quantise_k():
                quantise(nc, k, all_columns, k_grouped[:].rearrange("p r t -> p (r t)"))

            def score():
                for a in range(TILES):
                    scores[a] = psum_wide.tile([P, BLOCKS], F32, name="scores", tag="wide")
                    matmul_mx(nc, scores[a][:], q, slice(a * P, (a + 1) * P), k)

            def maxima(h):
                for a in (2 * h, 2 * h + 1):
                    nc.vector.tensor_reduce(
                        out=row_max[:, a : a + 1], in_=scores[a][:], axis=mybir.AxisListType.X, op=ALU.max
                    )
                pair = slice(2 * h, 2 * h + 2)
                nc.vector.tensor_scalar(
                    out=exp_bias[:, pair], in0=row_max[:, pair], scalar1=-SCALE, scalar2=None, op0=ALU.mult
                )

            def exponentials(h):
                for a in (2 * h, 2 * h + 1):
                    nc.scalar.activation(
                        out=e_bf16[:, a, :],
                        in_=scores[a][:],
                        func=ACT.Exp,
                        bias=exp_bias[:, a : a + 1],
                        scale=SCALE,
                        accum_out=row_sum[:, a : a + 1],
                    )

            def flip_e(h):
                words = e_bf16[:].bitcast(F32).rearrange("p a (u n) -> p a u n", u=2)
                grouped_words = e_grouped[:].bitcast(F32).rearrange("p (h a r) u -> p h a r u", h=2, a=2)
                flip_half(words[:, 2 * h : 2 * h + 2], grouped_words[:, h], by_scalar, "p a u r -> p a r u")

            def quantise_e():
                quantise(nc, e, all_columns, e_grouped[:].rearrange("p n t -> p (n t)"))
                nc.vector.reciprocal(out=inv_sum[:], in_=row_sum[:])

            def group_values(copy):
                copy(
                    out=vsum_grouped[:].rearrange("p (m i) (n e) -> p m n i e", i=RUN, e=2),
                    in_=vsum_bf16[b][:].rearrange("p (n e) (m i) -> p m n i e", i=RUN, e=2),
                )

            def quantise_values():
                quantise(nc, values, all_columns, vsum_grouped[:].rearrange("p c t -> p (c t)"))

            def mix(exits):
                for a in range(TILES):
                    mixed = psum_wide.tile([P, C], F32, name="mixed", tag="wide")
                    matmul_mx(nc, mixed[:], e, slice(a * P, (a + 1) * P), values)
                    result = store_pool.tile([P, C], F32, name="result")
                    if exits[a] == by_scalar:
                        nc.scalar.activation(out=result[:], in_=mixed[:], func=ACT.Copy, scale=inv_sum[:, a : a + 1])
                    else:
                        nc.vector.tensor_scalar(
                            out=result[:], in0=mixed[:], scalar1=inv_sum[:, a : a + 1], scalar2=None, op0=ALU.mult
                        )
                    nc.sync.dma_start(out=out[b].rearrange("(p a) c -> p a c", a=TILES)[:, a], in_=result[:])

            return {
                "flip_q": flip_q, "quantise_q": quantise_q, "flip_k": flip_k, "quantise_k": quantise_k,
                "score": score, "maxima": maxima, "exponentials": exponentials, "flip_e": flip_e,
                "quantise_e": quantise_e, "group_values": group_values, "quantise_values": quantise_values, "mix": mix,
            }

        bias_row = const.tile([P, C], BF16, name="bias_row")
        nc.vector.memset(bias_row[:], 0.0)
        nc.sync.dma_start(out=bias_row[0:1, :], in_=bv.unsqueeze(0))
        group_weights = const.tile([P, P], BF16, name="group_weights")
        nc.vector.memset(group_weights[:], float(GROUP))

        q_rows, k_rows = load_rows(q_blk[0], "(p a)"), load_rows(k_blk[0], "(a p)")
        wv_rows = load_rows(Wv, "(p a)")
        for c in range(2):
            for piece in range(2):
                load_chunk(c, piece, 2)
        for c in range(2, RAW_BUFS):
            load_chunk(c)

        warm = const.tile([P, 1], F32, name="warm")
        nc.vector.memset(warm[:], 0.0)
        nc.scalar.activation(out=warm[:], in_=warm[:], func=ACT.Exp)

        ident = const.tile([P, P], F32, name="ident")
        make_identity(nc, ident[:])

        group_bias = const.tile([P, C], F32, name="group_bias")
        spread = psum_vsum.tile([P, C], F32, name="spread", tag="vsum")
        nc.tensor.matmul(spread[:], lhsT=group_weights[:], rhs=bias_row[:], start=True, stop=True)
        nc.scalar.copy(out=group_bias[:], in_=spread[:])

        wv = mx_tiles(const, "wv", C)
        wv_grouped = const.tile([P, C, PACK], BF16, name="wv_grouped", align_bytes=64)
        vector_runs, scalar_runs = slice(0, VECTOR_RUNS), slice(VECTOR_RUNS, RUNS)
        one_each = (by_scalar, by_vector)

        first = attention(0, q_rows, k_rows, one_each)
        first["flip_q"]()
        first["quantise_q"]()
        first["flip_k"]()
        first["quantise_k"]()
        flip_weights(wv_rows, wv_grouped, one_each)
        first["score"]()
        first["maxima"](0)
        quantise(nc, wv, all_columns, wv_grouped[:].rearrange("p r t -> p (r t)"))
        for h in range(2):
            half = slice(h * P // 2, (h + 1) * P // 2)
            regroup(by_vector, 0, vector_runs, half)
            regroup(by_scalar, 0, scalar_runs, half)
            if h == 0:
                first["maxima"](1)
            first["exponentials"](h)
        load_chunk(RAW_BUFS)
        project(0, vector_runs)

        for c in range(1, LAST):
            if c == EVEN_OUT:
                regroup(by_vector, c, slice(0, 1))
                regroup(by_vector, c, slice(1, 2), slice(0, EVEN_GROUPS))
                regroup(by_scalar, c, slice(1, 2), slice(EVEN_GROUPS, P))
            else:
                regroup(by_vector, c, vector_runs)
            if c > 1:
                leave(c - 2)
            regroup(by_scalar, c, scalar_runs)

            if c == 1:
                first["flip_e"](0)
                first["flip_e"](1)
            if c == CHUNKS:
                last["flip_q"]()
            if c == CHUNKS + 1:
                last["quantise_q"]()
                last["flip_k"]()

            if c + RAW_BUFS < ALL_CHUNKS:
                load_chunk(c + RAW_BUFS)
            if c == 1:
                q_rows, k_rows = load_rows(q_blk[1], "(p a)"), load_rows(k_blk[1], "(a p)")
                last = attention(1, q_rows, k_rows, (by_scalar, by_scalar))

            if c == LAST - 1:
                last["quantise_k"]()
                last["score"]()
            project(c - 1, scalar_runs)
            project(c, vector_runs)

        regroup(by_vector, LAST, slice(0, 1))
        project(LAST - 1, scalar_runs)
        leave(LAST - 2)
        project(LAST, slice(0, 1))
        regroup(by_scalar, LAST, slice(1, RUNS))
        first["group_values"](by_scalar)
        last["maxima"](0)
        project(LAST, slice(1, 2))
        last["maxima"](1)
        last["exponentials"](0)
        last["exponentials"](1)
        project(LAST, slice(2, 3))
        leave(LAST - 1)
        project(LAST, slice(3, 4))
        last["flip_e"](0)
        last["flip_e"](1)
        first["quantise_e"]()
        first["quantise_values"]()
        leave(LAST)
        last["group_values"](by_vector)
        first["mix"]((by_scalar,) * TILES)
        last["quantise_e"]()
        last["quantise_values"]()
        last["mix"]((by_scalar, by_vector) * (TILES // 2))
